import numpy as np
import ml_dtypes


def mxq(x, axis, fmt="e4m3"):
    dtype, down = {"e4m3": (ml_dtypes.float8_e4m3fn, 7), "e5m2": (ml_dtypes.float8_e5m2, 14)}[fmt]
    v = np.moveaxis(np.asarray(x, np.float32).astype(ml_dtypes.bfloat16).astype(np.float64), axis, -1)
    blocks = v.reshape(v.shape[:-1] + (-1, 32))
    amax = np.abs(blocks).max(-1, keepdims=True)
    byte = np.maximum(np.where(amax > 0, np.frexp(amax)[1] - 1 + 127, 0) - down, 1)
    scale = np.exp2(byte - 127.0)
    codes = (blocks / scale).astype(np.float32).astype(dtype).astype(np.float64)
    return np.moveaxis((codes * scale).reshape(v.shape), -1, axis)


WIDE = False


def mx_kscale(k):
    if not WIDE:
        return np.ones(k)
    levels = np.array([10, -10, 5, -5, 0])
    a = np.random.permutation(np.resize(levels, k // 512 * 4)).reshape(k // 512, 4)
    idx = np.arange(k)
    return np.exp2(a[idx // 512, idx % 128 // 32])


BF16 = ml_dtypes.bfloat16


def bf(x):
    return np.asarray(x, np.float32).astype(BF16)


def f64(x):
    return np.asarray(x).astype(np.float64)


NQ, NK, QS, KS, F, DEG = 4096, 1024, 512, 512, 512, 32


def setup_inputs():
    s = mx_kscale(F)
    return {"A": bf(np.random.random((NQ, NK)) < DEG / NK),
            "qe1": bf(np.random.standard_normal((NQ, F)) * s),
            "ke1": bf(np.random.standard_normal((NK, F)) / s),
            "ve1": bf(np.random.standard_normal((NK, F)) * 2.0)}


def reference(A, qe1, ke1, ve1):
    prod = (mxq(f64(qe1), 1, "e4m3") @ mxq(f64(ke1), 1, "e4m3").T) / np.sqrt(F)
    masked = f64(A) * prod
    e = np.exp(masked - masked.max(axis=1, keepdims=True))
    return (mxq(e, 1, "e4m3") @ mxq(f64(ve1), 0, "e4m3")) / e.sum(axis=1, keepdims=True)

@@ -1,0 +1,251 @@
+from contextlib import ExitStack
+import math
+
+import concourse.bass as bass
+import concourse.mybir as mybir
+import concourse.tile as tile
+from concourse.masks import make_identity
+
+F32 = mybir.dt.float32
+BF16 = mybir.dt.bfloat16
+U32 = mybir.dt.uint32
+U8 = mybir.dt.uint8
+FP8X4 = mybir.dt.float8_e4m3fn_x4
+ALU = mybir.AluOpType
+ACT = mybir.ActivationFunctionType
+AX = mybir.AxisListType
+
+P = 128
+NQ, NK, F = 4096, 1024, 512
+NT = NQ // P
+FLOPS = 2 * NQ * NK * F * 2
+PIN = True
+
+
+def tile_attention_prop_pb_t_kernel(tc, A, qe1, ke1, ve1, out):
+    nc = tc.nc
+    inv_sqrt_f = 1.0 / math.sqrt(F)
+    with ExitStack() as ctx:
+        if PIN:
+            ctx.enter_context(tc.manual_schedule())
+        keep = ctx.enter_context(tc.tile_pool(name="keep", bufs=1))
+        work = ctx.enter_context(tc.tile_pool(name="work", bufs=3))
+        small = ctx.enter_context(tc.tile_pool(name="small", bufs=4))
+        outp = ctx.enter_context(tc.tile_pool(name="outp", bufs=4))
+        ps_s = ctx.enter_context(tc.psum_pool(name="ps_s", bufs=4))
+        ps_et = ctx.enter_context(tc.psum_pool(name="ps_et", bufs=2))
+        ps_o = ctx.enter_context(tc.psum_pool(name="ps_o", bufs=1))
+        ps_qt = ctx.enter_context(tc.psum_pool(name="ps_qt", bufs=1))
+
+        warm = keep.tile([P, 1], F32, name="warm")
+        nc.vector.memset(warm[:], 0.0)
+        warm2 = keep.tile([P, 1], F32, name="warm2")
+        nc.scalar.activation(out=warm2[:], in_=warm[:], func=ACT.Exp)
+        ident_f = keep.tile([P, P], F32, name="ident_f")
+        make_identity(nc, ident_f[:])
+        ident_b = keep.tile([P, P], BF16, name="ident_b")
+        make_identity(nc, ident_b[:])
+
+        q_view = qe1.rearrange("(p n) f -> p n f", n=NT)
+        a_view = A.rearrange("(p n) k -> p n k", n=NT)
+        o_view = out.rearrange("(p n) f -> p n f", n=NT)
+        q_sb = [keep.tile([P, 4, F], BF16, name="q_sb%d" % c) for c in range(NT // 4)]
+        a_sb = [keep.tile([P, 2, NK], BF16, name="a_sb%d" % c) for c in range(NT // 2)]
+        k_sb = keep.tile([P, 8, F], BF16, name="k_sb")
+        v_sb = keep.tile([P, 8, F], BF16, name="v_sb")
+        k_view = ke1.rearrange("(j p) f -> p j f", p=P)
+        v_view = ve1.rearrange("(j p) f -> p j f", p=P)
+
+        def load_q(c):
+            nc.sync.dma_start(out=q_sb[c][:], in_=q_view[:, 4 * c:4 * c + 4, :])
+
+        def load_a(c):
+            nc.sync.dma_start(out=a_sb[c][:], in_=a_view[:, 2 * c:2 * c + 2, :])
+
+        load_q(0)
+        nc.sync.dma_start(out=k_sb[:, 0:4, :], in_=k_view[:, 0:4, :])
+        nc.sync.dma_start(out=k_sb[:, 4:8, :], in_=k_view[:, 4:8, :])
+        load_a(0)
+        nc.sync.dma_start(out=v_sb[:], in_=v_view)
+        load_a(1)
+        for c in range(1, NT // 4):
+            load_q(c)
+            load_a(2 * c)
+            load_a(2 * c + 1)
+
+        k_codes = keep.tile([P, NK], U32, name="k_codes", align_bytes=64)
+        k_scales = keep.tile([P, NK], U8, name="k_scales", align_bytes=64)
+        v_codes = keep.tile([P, 2 * F], U32, name="v_codes", align_bytes=64)
+        v_scales = keep.tile([P, 2 * F], U8, name="v_scales", align_bytes=64)
+        q_codes = [keep.tile([P, 2 * P], U32, name="q_codes%d" % j, align_bytes=64) for j in range(NT // 2)]
+        q_scales = [keep.tile([P, 2 * P], U8, name="q_scales%d" % j, align_bytes=64) for j in range(NT // 2)]
+        kg = keep.tile([P, NK * 4], BF16, name="kg", align_bytes=64)
+        vg = keep.tile([P, 2 * F * 4], BF16, name="vg", align_bytes=64)
+
+        qg = {}
+        qt = {}
+
+        def q_transpose(j):
+            qt[j] = ps_qt.tile([P, 2, 2, P], F32, name="qt")
+            for a in range(2):
+                n = 2 * j + a
+                words = q_sb[n // 4][:, n % 4, :].bitcast(F32)
+                for u in range(2):
+                    nc.tensor.transpose(qt[j][:, a, u, :], words[:, P * u:P * u + P], ident_f[:])
+
+        def q_evacuate(j):
+            qg[j] = work.tile([P, 2 * P * 4], BF16, name="qg", align_bytes=64)
+            nc.vector.tensor_copy(
+                out=qg[j][:].bitcast(F32).rearrange("p (a q u) -> p a q u", a=2, u=2),
+                in_=qt[j][:].rearrange("p a u q -> p a q u"),
+            )
+
+        def q_quantise(j):
+            nc.vector.quantize_mx(out=q_codes[j][:].bitcast(FP8X4), scales=q_scales[j][:], in_=qg[j][:])
+
+        q_transpose(0)
+        q_evacuate(0)
+        kg_words = kg[:].bitcast(F32).rearrange("p (b a k u) -> p b a k u", b=4, a=2, u=2)
+        for b in range(4):
+            kt = ps_s.tile([P, 2, 2, P], F32, name="kt", tag="s")
+            for a in range(2):
+                words = k_sb[:, 2 * b + a, :].bitcast(F32)
+                for u in range(2):
+                    nc.tensor.transpose(kt[:, a, u, :], words[:, P * u:P * u + P], ident_f[:])
+            src = kt[:].rearrange("p a u k -> p a k u")
+            if b % 2 == 0:
+                nc.scalar.copy(out=kg_words[:, b], in_=src)
+            else:
+                nc.vector.tensor_copy(out=kg_words[:, b], in_=src)
+        q_quantise(0)
+        for g in range(2):
+            nc.vector.quantize_mx(
+                out=k_codes[:, 512 * g:512 * g + 512].bitcast(FP8X4),
+                scales=k_scales[:, 512 * g:512 * g + 512],
+                in_=kg[:, 2048 * g:2048 * g + 2048],
+            )
+        q_transpose(1)
+        q_evacuate(1)
+        q_quantise(1)
+
+        vg_view = vg[:].rearrange("p (g f t) -> p g f t", g=2, t=4)
+
+        def v_regroup(g):
+            nc.scalar.copy(out=vg_view[:, g], in_=v_sb[:, 4 * g:4 * g + 4, :].rearrange("p t f -> p f t"))
+
+        def v_quantise(g):
+            nc.vector.quantize_mx(
+                out=v_codes[:, 512 * g:512 * g + 512].bitcast(FP8X4),
+                scales=v_scales[:, 512 * g:512 * g + 512],
+                in_=vg[:, 2048 * g:2048 * g + 2048],
+            )
+
+        s_ps, m_sb, nmx, rs, e_sb, et_ps = {}, {}, {}, {}, {}, {}
+        eg, ec, es, rr, o_ps, o_sb = {}, {}, {}, {}, {}, {}
+
+        def scores(i):
+            s_ps[i] = []
+            for g in range(2):
+                s = ps_s.tile([P, 512], F32, name="s", tag="s")
+                nc.tensor.matmul_mx(
+                    out=s[:],
+                    lhsT=q_codes[i // 2][:, P * (i % 2):P * (i % 2) + P].bitcast(FP8X4),
+                    lhsT_scale=q_scales[i // 2][:, P * (i % 2):P * (i % 2) + P],
+                    rhs=k_codes[:, 512 * g:512 * g + 512].bitcast(FP8X4),
+                    rhs_scale=k_scales[:, 512 * g:512 * g + 512],
+                    start=True,
+                    stop=True,
+                )
+                s_ps[i].append(s)
+
+        def mask_and_max(i):
+            m_sb[i] = work.tile([P, NK], F32, name="m")
+            for g in range(2):
+                nc.vector.scalar_tensor_tensor(
+                    out=m_sb[i][:, 512 * g:512 * g + 512],
+                    in0=s_ps[i][g][:],
+                    scalar=-inv_sqrt_f,
+                    in1=a_sb[i // 2][:, i % 2, 512 * g:512 * g + 512],
+                    op0=ALU.mult,
+                    op1=ALU.mult,
+                )
+            nmx[i] = small.tile([P, 1], F32, name="nmx")
+            nc.vector.tensor_reduce(out=nmx[i][:], in_=m_sb[i][:], axis=AX.X, op=ALU.min)
+
+        def exponent(i):
+            e_sb[i] = work.tile([P, NK], BF16, name="e")
+            rs[i] = small.tile([P, 1], F32, name="rs")
+            nc.scalar.activation(out=e_sb[i][:], in_=m_sb[i][:], func=ACT.Exp, bias=nmx[i][:, 0:1], scale=-1.0,
+                                 accum_out=rs[i][:, 0:1])
+
+        def e_transpose(i):
+            et_ps[i] = ps_et.tile([P, 8, P], BF16, name="et")
+            for j in range(8):
+                nc.tensor.transpose(et_ps[i][:, j, :], e_sb[i][:, P * j:P * j + P], ident_b[:])
+
+        def e_evacuate(i):
+            eg[i] = work.tile([P, NK], BF16, name="eg", align_bytes=64)
+            nc.scalar.copy(
+                out=eg[i][:].rearrange("p (g q t) -> p g q t", g=2, t=4),
+                in_=et_ps[i][:].rearrange("p (g t) q -> p g q t", t=4),
+            )
+
+        def e_quantise(i):
+            ec[i] = work.tile([P, 2 * P], U32, name="ec", align_bytes=64)
+            es[i] = work.tile([P, 2 * P], U8, name="es", align_bytes=64)
+            nc.vector.quantize_mx(out=ec[i][:].bitcast(FP8X4), scales=es[i][:], in_=eg[i][:])
+            rr[i] = small.tile([P, 1], F32, name="rr")
+            nc.vector.reciprocal(out=rr[i][:], in_=rs[i][:])
+
+        def weighted_sum(i):
+            o_ps[i] = ps_o.tile([P, F], F32, name="o")
+            for g in range(2):
+                nc.tensor.matmul_mx(
+                    out=o_ps[i][:],
+                    lhsT=ec[i][:, P * g:P * g + P].bitcast(FP8X4),
+                    lhsT_scale=es[i][:, P * g:P * g + P],
+                    rhs=v_codes[:, 512 * g:512 * g + 512].bitcast(FP8X4),
+                    rhs_scale=v_scales[:, 512 * g:512 * g + 512],
+                    start=(g == 0),
+                    stop=(g == 1),
+                )
+
+        def normalise_and_store(i):
+            if i % 2 == 0:
+                o_sb[i // 2] = outp.tile([P, 2, F], F32, name="o_sb")
+            nc.scalar.activation(out=o_sb[i // 2][:, i % 2, :], in_=o_ps[i][:], func=ACT.Copy, scale=rr[i][:, 0:1])
+            if i % 2 == 1:
+                nc.sync.dma_start(out=o_view[:, i - 1:i + 1, :], in_=o_sb[i // 2][:])
+
+        scores(0)
+        scores(1)
+        v_regroup(0)
+
+        for i in range(NT + 2):
+            if 0 <= i - 1 < NT:
+                e_transpose(i - 1)
+            if i % 2 == 0 and (i + 4) // 2 < NT // 2:
+                q_transpose((i + 4) // 2)
+            if i < NT:
+                mask_and_max(i)
+            if i % 2 == 0 and (i + 4) // 2 < NT // 2:
+                q_evacuate((i + 4) // 2)
+            if i % 2 == 1 and (i + 3) // 2 < NT // 2:
+                q_quantise((i + 3) // 2)
+            if i == 1:
+                v_quantise(0)
+                v_quantise(1)
+            if 0 <= i - 2 < NT:
+                e_quantise(i - 2)
+            if i + 2 < NT:
+                scores(i + 2)
+            if 0 <= i - 2 < NT:
+                weighted_sum(i - 2)
+            if i < NT:
+                exponent(i)
+            if i == 0:
+                v_regroup(1)
+            if 0 <= i - 1 < NT:
+                e_evacuate(i - 1)
+            if 0 <= i - 2 < NT:
+                normalise_and_store(i - 2)

@@ -1,9 +1,7 @@
 from contextlib import ExitStack
 import math
 
-import concourse.bass as bass
 import concourse.mybir as mybir
-import concourse.tile as tile
 from concourse.masks import make_identity
 
 F32 = mybir.dt.float32
@@ -18,6 +16,7 @@ AX = mybir.AxisListType
 P = 128
 NQ, NK, F = 4096, 1024, 512
 NT = NQ // P
+NPAIR = NT // 2
 FLOPS = 2 * NQ * NK * F * 2
 PIN = True
 
@@ -30,108 +29,122 @@ def tile_attention_prop_pb_t_kernel(tc, A, qe1, ke1, ve1, out):
             ctx.enter_context(tc.manual_schedule())
         keep = ctx.enter_context(tc.tile_pool(name="keep", bufs=1))
         work = ctx.enter_context(tc.tile_pool(name="work", bufs=3))
-        small = ctx.enter_context(tc.tile_pool(name="small", bufs=4))
+        small = ctx.enter_context(tc.tile_pool(name="small", bufs=8))
         outp = ctx.enter_context(tc.tile_pool(name="outp", bufs=4))
-        ps_s = ctx.enter_context(tc.psum_pool(name="ps_s", bufs=4))
+        ps_s = ctx.enter_context(tc.psum_pool(name="ps_s", bufs=3))
         ps_et = ctx.enter_context(tc.psum_pool(name="ps_et", bufs=2))
-        ps_o = ctx.enter_context(tc.psum_pool(name="ps_o", bufs=1))
+        ps_o = ctx.enter_context(tc.psum_pool(name="ps_o", bufs=2))
         ps_qt = ctx.enter_context(tc.psum_pool(name="ps_qt", bufs=1))
 
-        warm = keep.tile([P, 1], F32, name="warm")
-        nc.vector.memset(warm[:], 0.0)
-        warm2 = keep.tile([P, 1], F32, name="warm2")
-        nc.scalar.activation(out=warm2[:], in_=warm[:], func=ACT.Exp)
         ident_f = keep.tile([P, P], F32, name="ident_f")
         make_identity(nc, ident_f[:])
         ident_b = keep.tile([P, P], BF16, name="ident_b")
         make_identity(nc, ident_b[:])
+        warm = keep.tile([P, 1], F32, name="warm")
+        nc.vector.memset(warm[:], 0.0)
+        warm2 = keep.tile([P, 1], F32, name="warm2")
+        nc.scalar.activation(out=warm2[:], in_=warm[:], func=ACT.Exp)
 
         q_view = qe1.rearrange("(p n) f -> p n f", n=NT)
         a_view = A.rearrange("(p n) k -> p n k", n=NT)
         o_view = out.rearrange("(p n) f -> p n f", n=NT)
-        q_sb = [keep.tile([P, 4, F], BF16, name="q_sb%d" % c) for c in range(NT // 4)]
-        a_sb = [keep.tile([P, 2, NK], BF16, name="a_sb%d" % c) for c in range(NT // 2)]
+        q_sb = [keep.tile([P, 2, F], BF16, name="q_sb%d" % c) for c in range(NPAIR)]
+        a_sb = [keep.tile([P, 2, NK], BF16, name="a_sb%d" % c) for c in range(NPAIR)]
         k_sb = keep.tile([P, 8, F], BF16, name="k_sb")
         v_sb = keep.tile([P, 8, F], BF16, name="v_sb")
         k_view = ke1.rearrange("(j p) f -> p j f", p=P)
         v_view = ve1.rearrange("(j p) f -> p j f", p=P)
 
         def load_q(c):
-            nc.sync.dma_start(out=q_sb[c][:], in_=q_view[:, 4 * c:4 * c + 4, :])
+            nc.sync.dma_start(out=q_sb[c][:], in_=q_view[:, 2 * c:2 * c + 2, :])
 
         def load_a(c):
             nc.sync.dma_start(out=a_sb[c][:], in_=a_view[:, 2 * c:2 * c + 2, :])
 
+        def load_k(b):
+            nc.sync.dma_start(out=k_sb[:, 2 * b:2 * b + 2, :], in_=k_view[:, 2 * b:2 * b + 2, :])
+
+        load_k(0)
+        load_k(1)
         load_q(0)
-        nc.sync.dma_start(out=k_sb[:, 0:4, :], in_=k_view[:, 0:4, :])
-        nc.sync.dma_start(out=k_sb[:, 4:8, :], in_=k_view[:, 4:8, :])
-        load_a(0)
+        load_k(2)
+        load_k(3)
+        nc.sync.dma_start(out=a_sb[0][:, 0, :], in_=a_view[:, 0, :])
+        load_q(1)
         nc.sync.dma_start(out=v_sb[:], in_=v_view)
-        load_a(1)
-        for c in range(1, NT // 4):
-            load_q(c)
-            load_a(2 * c)
-            load_a(2 * c + 1)
+        nc.sync.dma_start(out=a_sb[0][:, 1, :], in_=a_view[:, 1, :])
+        load_q(2)
+        for c in range(1, NPAIR):
+            load_a(c)
+            if c + 2 < NPAIR:
+                load_q(c + 2)
 
         k_codes = keep.tile([P, NK], U32, name="k_codes", align_bytes=64)
         k_scales = keep.tile([P, NK], U8, name="k_scales", align_bytes=64)
         v_codes = keep.tile([P, 2 * F], U32, name="v_codes", align_bytes=64)
         v_scales = keep.tile([P, 2 * F], U8, name="v_scales", align_bytes=64)
-        q_codes = [keep.tile([P, 2 * P], U32, name="q_codes%d" % j, align_bytes=64) for j in range(NT // 2)]
-        q_scales = [keep.tile([P, 2 * P], U8, name="q_scales%d" % j, align_bytes=64) for j in range(NT // 2)]
+        q_codes = [keep.tile([P, 2 * P], U32, name="q_codes%d" % j, align_bytes=64) for j in range(NPAIR)]
+        q_scales = [keep.tile([P, 2 * P], U8, name="q_scales%d" % j, align_bytes=64) for j in range(NPAIR)]
         kg = keep.tile([P, NK * 4], BF16, name="kg", align_bytes=64)
         vg = keep.tile([P, 2 * F * 4], BF16, name="vg", align_bytes=64)
+
+        def copy_on(eng, dst, src):
+            if eng == "v":
+                nc.vector.tensor_copy(out=dst, in_=src)
+            else:
+                nc.scalar.copy(out=dst, in_=src)
 
         qg = {}
         qt = {}
 
-        def q_transpose(j):
-            qt[j] = ps_qt.tile([P, 2, 2, P], F32, name="qt")
+        def q_transpose(j, borrow=False):
+            if borrow:
+                qt[j] = ps_o.tile([P, 2, 2, P], F32, name="qt_o", tag="o")
+            else:
+                qt[j] = ps_qt.tile([P, 2, 2, P], F32, name="qt")
             for a in range(2):
-                n = 2 * j + a
-                words = q_sb[n // 4][:, n % 4, :].bitcast(F32)
+                words = q_sb[j][:, a, :].bitcast(F32)
                 for u in range(2):
                     nc.tensor.transpose(qt[j][:, a, u, :], words[:, P * u:P * u + P], ident_f[:])
 
-        def q_evacuate(j):
+        def q_evacuate(j, eng):
             qg[j] = work.tile([P, 2 * P * 4], BF16, name="qg", align_bytes=64)
-            nc.vector.tensor_copy(
-                out=qg[j][:].bitcast(F32).rearrange("p (a q u) -> p a q u", a=2, u=2),
-                in_=qt[j][:].rearrange("p a u q -> p a q u"),
-            )
+            copy_on(eng, qg[j][:].bitcast(F32).rearrange("p (a q u) -> p a q u", a=2, u=2),
+                    qt[j][:].rearrange("p a u q -> p a q u"))
 
         def q_quantise(j):
             nc.vector.quantize_mx(out=q_codes[j][:].bitcast(FP8X4), scales=q_scales[j][:], in_=qg[j][:])
 
-        q_transpose(0)
-        q_evacuate(0)
         kg_words = kg[:].bitcast(F32).rearrange("p (b a k u) -> p b a k u", b=4, a=2, u=2)
-        for b in range(4):
-            kt = ps_s.tile([P, 2, 2, P], F32, name="kt", tag="s")
+        kt = {}
+
+        def k_transpose(b):
+            kt[b] = ps_s.tile([P, 2, 2, P], F32, name="kt", tag="s")
             for a in range(2):
                 words = k_sb[:, 2 * b + a, :].bitcast(F32)
                 for u in range(2):
-                    nc.tensor.transpose(kt[:, a, u, :], words[:, P * u:P * u + P], ident_f[:])
-            src = kt[:].rearrange("p a u k -> p a k u")
-            if b % 2 == 0:
-                nc.scalar.copy(out=kg_words[:, b], in_=src)
-            else:
-                nc.vector.tensor_copy(out=kg_words[:, b], in_=src)
-        q_quantise(0)
-        for g in range(2):
+                    nc.tensor.transpose(kt[b][:, a, u, :], words[:, P * u:P * u + P], ident_f[:])
+
+        def k_evacuate(b, eng):
+            copy_on(eng, kg_words[:, b], kt[b][:].rearrange("p a u k -> p a k u"))
+
+        def k_quantise(b):
             nc.vector.quantize_mx(
-                out=k_codes[:, 512 * g:512 * g + 512].bitcast(FP8X4),
-                scales=k_scales[:, 512 * g:512 * g + 512],
-                in_=kg[:, 2048 * g:2048 * g + 2048],
+                out=k_codes[:, 256 * b:256 * b + 256].bitcast(FP8X4),
+                scales=k_scales[:, 256 * b:256 * b + 256],
+                in_=kg[:, 1024 * b:1024 * b + 1024],
             )
-        q_transpose(1)
-        q_evacuate(1)
-        q_quantise(1)
 
-        vg_view = vg[:].rearrange("p (g f t) -> p g f t", g=2, t=4)
-
-        def v_regroup(g):
-            nc.scalar.copy(out=vg_view[:, g], in_=v_sb[:, 4 * g:4 * g + 4, :].rearrange("p t f -> p f t"))
+        def v_regroup(g, h, eng):
+            c0 = 2048 * g + 1024 * h
+            dst = vg[:, c0:c0 + 1024].rearrange("p (c i t) -> p c t i", i=4, t=4)
+            src = v_sb[:, 4 * g:4 * g + 4, 256 * h:256 * h + 256].rearrange("p t (c i) -> p c t i", i=4)
+            if eng == "g":
+                dst = vg[:, c0:c0 + 1024].rearrange("p (f t) -> p f t", t=4)
+                src = v_sb[:, 4 * g:4 * g + 4, 256 * h:256 * h + 256].rearrange("p t f -> p f t")
+                nc.gpsimd.tensor_scalar(out=dst, in0=src, scalar1=1.0, scalar2=0.0, op0=ALU.mult, op1=ALU.add)
+            else:
+                copy_on(eng, dst, src)
 
         def v_quantise(g):
             nc.vector.quantize_mx(
@@ -140,35 +153,35 @@ def tile_attention_prop_pb_t_kernel(tc, A, qe1, ke1, ve1, out):
                 in_=vg[:, 2048 * g:2048 * g + 2048],
             )
 
-        s_ps, m_sb, nmx, rs, e_sb, et_ps = {}, {}, {}, {}, {}, {}
+        s_ps, m_sb, nmx, rs, e_sb, et_ps, ex = {}, {}, {}, {}, {}, {}, {}
         eg, ec, es, rr, o_ps, o_sb = {}, {}, {}, {}, {}, {}
 
-        def scores(i):
-            s_ps[i] = []
-            for g in range(2):
-                s = ps_s.tile([P, 512], F32, name="s", tag="s")
-                nc.tensor.matmul_mx(
-                    out=s[:],
-                    lhsT=q_codes[i // 2][:, P * (i % 2):P * (i % 2) + P].bitcast(FP8X4),
-                    lhsT_scale=q_scales[i // 2][:, P * (i % 2):P * (i % 2) + P],
-                    rhs=k_codes[:, 512 * g:512 * g + 512].bitcast(FP8X4),
-                    rhs_scale=k_scales[:, 512 * g:512 * g + 512],
-                    start=True,
-                    stop=True,
-                )
-                s_ps[i].append(s)
+        def scores(i, g):
+            s = ps_s.tile([P, 512], F32, name="s", tag="s")
+            nc.tensor.matmul_mx(
+                out=s[:],
+                lhsT=q_codes[i // 2][:, P * (i % 2):P * (i % 2) + P].bitcast(FP8X4),
+                lhsT_scale=q_scales[i // 2][:, P * (i % 2):P * (i % 2) + P],
+                rhs=k_codes[:, 512 * g:512 * g + 512].bitcast(FP8X4),
+                rhs_scale=k_scales[:, 512 * g:512 * g + 512],
+                start=True,
+                stop=True,
+            )
+            s_ps[(i, g)] = s
 
-        def mask_and_max(i):
-            m_sb[i] = work.tile([P, NK], F32, name="m")
-            for g in range(2):
-                nc.vector.scalar_tensor_tensor(
-                    out=m_sb[i][:, 512 * g:512 * g + 512],
-                    in0=s_ps[i][g][:],
-                    scalar=-inv_sqrt_f,
-                    in1=a_sb[i // 2][:, i % 2, 512 * g:512 * g + 512],
-                    op0=ALU.mult,
-                    op1=ALU.mult,
-                )
+        def mask(i, g):
+            if g == 0:
+                m_sb[i] = work.tile([P, NK], F32, name="m")
+            nc.vector.scalar_tensor_tensor(
+                out=m_sb[i][:, 512 * g:512 * g + 512],
+                in0=s_ps[(i, g)][:],
+                scalar=-inv_sqrt_f,
+                in1=a_sb[i // 2][:, i % 2, 512 * g:512 * g + 512],
+                op0=ALU.mult,
+                op1=ALU.mult,
+            )
+
+        def row_max(i):
             nmx[i] = small.tile([P, 1], F32, name="nmx")
             nc.vector.tensor_reduce(out=nmx[i][:], in_=m_sb[i][:], axis=AX.X, op=ALU.min)
 
@@ -178,17 +191,43 @@ def tile_attention_prop_pb_t_kernel(tc, A, qe1, ke1, ve1, out):
             nc.scalar.activation(out=e_sb[i][:], in_=m_sb[i][:], func=ACT.Exp, bias=nmx[i][:, 0:1], scale=-1.0,
                                  accum_out=rs[i][:, 0:1])
 
-        def e_transpose(i):
-            et_ps[i] = ps_et.tile([P, 8, P], BF16, name="et")
+        def e_transpose(i, banks):
+            per = 8 // banks
+            et_ps[i] = [ps_et.tile([P, per, P], BF16, name="et")]
+            if banks == 2:
+                et_ps[i].append(ps_s.tile([P, per, P], BF16, name="et_s", tag="s"))
             for j in range(8):
-                nc.tensor.transpose(et_ps[i][:, j, :], e_sb[i][:, P * j:P * j + P], ident_b[:])
+                nc.tensor.transpose(et_ps[i][j // per][:, j % per, :], e_sb[i][:, P * j:P * j + P], ident_b[:])
 
         def e_evacuate(i):
-            eg[i] = work.tile([P, NK], BF16, name="eg", align_bytes=64)
-            nc.scalar.copy(
+            ex[i] = work.tile([P, 8, P], BF16, name="ex")
+            nc.scalar.copy(out=ex[i][:], in_=et_ps[i][0][:])
+
+        def e_regroup(i):
+            eg[i] = work.tile([P, NK], BF16, name="eg", align_bytes=64, bufs=1)
+            if i == 0:
+                nc.vector.memset(eg[i][:, 0:2], 0.0)
+            nc.gpsimd.tensor_scalar(
                 out=eg[i][:].rearrange("p (g q t) -> p g q t", g=2, t=4),
-                in_=et_ps[i][:].rearrange("p (g t) q -> p g q t", t=4),
+                in0=ex[i][:].rearrange("p (g t) q -> p g q t", t=4),
+                scalar1=1.0, scalar2=0.0, op0=ALU.mult, op1=ALU.add,
             )
+
+        def e_regroup_on_vector(i):
+            eg[i] = work.tile([P, NK], BF16, name="eg", align_bytes=64, bufs=1)
+            nc.vector.tensor_copy(
+                out=eg[i][:].rearrange("p (g q t) -> p g q t", g=2, t=4),
+                in_=ex[i][:].rearrange("p (g t) q -> p g q t", t=4),
+            )
+
+        def e_evacuate_regrouped(i, engines):
+            eg[i] = work.tile([P, NK], BF16, name="eg", align_bytes=64, bufs=1)
+            dst = eg[i][:].rearrange("p (g q t) -> p g q t", g=2, t=4)
+            if len(engines) == 1:
+                copy_on(engines[0], dst, et_ps[i][0][:].rearrange("p (g t) q -> p g q t", t=4))
+            else:
+                for g in range(2):
+                    copy_on(engines[g], dst[:, g], et_ps[i][g][:].rearrange("p t q -> p q t"))
 
         def e_quantise(i):
             ec[i] = work.tile([P, 2 * P], U32, name="ec", align_bytes=64)
@@ -197,55 +236,123 @@ def tile_attention_prop_pb_t_kernel(tc, A, qe1, ke1, ve1, out):
             rr[i] = small.tile([P, 1], F32, name="rr")
             nc.vector.reciprocal(out=rr[i][:], in_=rs[i][:])
 
-        def weighted_sum(i):
-            o_ps[i] = ps_o.tile([P, F], F32, name="o")
-            for g in range(2):
-                nc.tensor.matmul_mx(
-                    out=o_ps[i][:],
-                    lhsT=ec[i][:, P * g:P * g + P].bitcast(FP8X4),
-                    lhsT_scale=es[i][:, P * g:P * g + P],
-                    rhs=v_codes[:, 512 * g:512 * g + 512].bitcast(FP8X4),
-                    rhs_scale=v_scales[:, 512 * g:512 * g + 512],
-                    start=(g == 0),
-                    stop=(g == 1),
-                )
+        def weighted_sum(i, banks):
+            width = F // banks
+            if banks == 1:
+                o_ps[i] = [ps_o.tile([P, F], F32, name="o")]
+            else:
+                o_ps[i] = [ps_s.tile([P, width], F32, name="o_half", tag="s") for h in range(banks)]
+            for h in range(banks):
+                for g in range(2):
+                    c0 = 512 * g + width * h
+                    nc.tensor.matmul_mx(
+                        out=o_ps[i][h][:],
+                        lhsT=ec[i][:, P * g:P * g + P].bitcast(FP8X4),
+                        lhsT_scale=es[i][:, P * g:P * g + P],
+                        rhs=v_codes[:, c0:c0 + width].bitcast(FP8X4),
+                        rhs_scale=v_scales[:, c0:c0 + width],
+                        start=(g == 0),
+                        stop=(g == 1),
+                    )
 
-        def normalise_and_store(i):
+        def normalise(i, engines):
             if i % 2 == 0:
                 o_sb[i // 2] = outp.tile([P, 2, F], F32, name="o_sb")
-            nc.scalar.activation(out=o_sb[i // 2][:, i % 2, :], in_=o_ps[i][:], func=ACT.Copy, scale=rr[i][:, 0:1])
-            if i % 2 == 1:
-                nc.sync.dma_start(out=o_view[:, i - 1:i + 1, :], in_=o_sb[i // 2][:])
+            width = F // len(engines)
+            for h in range(len(engines)):
+                dst = o_sb[i // 2][:, i % 2, width * h:width * h + width]
+                if engines[h] == "v":
+                    nc.vector.tensor_scalar(out=dst, in0=o_ps[i][h][:], scalar1=rr[i][:, 0:1], scalar2=None, op0=ALU.mult)
+                else:
+                    nc.scalar.activation(out=dst, in_=o_ps[i][h][:], func=ACT.Copy, scale=rr[i][:, 0:1])
 
-        scores(0)
-        scores(1)
-        v_regroup(0)
+        def store(first, count):
+            nc.sync.dma_start(out=o_view[:, first:first + count, :], in_=o_sb[first // 2][:, first % 2:first % 2 + count, :])
 
-        for i in range(NT + 2):
-            if 0 <= i - 1 < NT:
-                e_transpose(i - 1)
-            if i % 2 == 0 and (i + 4) // 2 < NT // 2:
-                q_transpose((i + 4) // 2)
-            if i < NT:
-                mask_and_max(i)
-            if i % 2 == 0 and (i + 4) // 2 < NT // 2:
-                q_evacuate((i + 4) // 2)
-            if i % 2 == 1 and (i + 3) // 2 < NT // 2:
-                q_quantise((i + 3) // 2)
-            if i == 1:
-                v_quantise(0)
-                v_quantise(1)
-            if 0 <= i - 2 < NT:
-                e_quantise(i - 2)
-            if i + 2 < NT:
-                scores(i + 2)
-            if 0 <= i - 2 < NT:
-                weighted_sum(i - 2)
-            if i < NT:
-                exponent(i)
+        k_transpose(0)
+        k_transpose(1)
+        q_transpose(0)
+        k_evacuate(0, "s")
+        k_evacuate(1, "v")
+        q_evacuate(0, "s")
+        k_quantise(0)
+        k_transpose(2)
+        k_evacuate(2, "v")
+        k_quantise(1)
+        q_quantise(0)
+        k_transpose(3)
+        q_transpose(1)
+        scores(0, 0)
+        k_evacuate(3, "s")
+        q_evacuate(1, "s")
+        k_quantise(2)
+        k_quantise(3)
+        scores(0, 1)
+        scores(1, 0)
+        v_regroup(0, 0, "s")
+        q_transpose(2, borrow=True)
+
+        def live(x):
+            return 0 <= x < NT
+
+        for i in range(NT):
+            mask(i, 0)
             if i == 0:
-                v_regroup(1)
-            if 0 <= i - 1 < NT:
+                q_quantise(1)
+                nc.vector.memset(vg[:, 2048:2050], 0.0)
+                v_regroup(1, 0, "g")
+                v_regroup(1, 1, "g")
+            if live(i + 1):
+                scores(i + 1, 1)
+            mask(i, 1)
+            if i == 2:
+                q_quantise(2)
+            if i % 2 == 1 and i > 1 and (i + 3) // 2 < NPAIR:
+                q_quantise((i + 3) // 2)
+            if i == 2 or i == 3:
+                v_quantise(i - 2)
+            if live(i - 4):
+                e_quantise(i - 4)
+            if live(i - 3):
+                e_regroup(i - 3)
+            if live(i + 2):
+                scores(i + 2, 0)
+            if live(i - 1):
+                e_transpose(i - 1, 1)
+            if i % 2 == 0 and (i + 6) // 2 < NPAIR:
+                q_transpose((i + 6) // 2)
+            if live(i - 4):
+                weighted_sum(i - 4, 1)
+            row_max(i)
+            exponent(i)
+            if i == 0:
+                q_evacuate(2, "s")
+                v_regroup(0, 1, "s")
+            if live(i - 1) and i - 1 < NT - 2:
                 e_evacuate(i - 1)
-            if 0 <= i - 2 < NT:
-                normalise_and_store(i - 2)
+            if live(i - 4):
+                normalise(i - 4, ["s"])
+                if (i - 4) % 2 == 1:
+                    store(i - 5, 2)
+            if i % 2 == 0 and (i + 6) // 2 < NPAIR:
+                q_evacuate((i + 6) // 2, "s")
+
+        e_quantise(NT - 4)
+        e_regroup_on_vector(NT - 3)
+        weighted_sum(NT - 4, 1)
+        e_transpose(NT - 1, 2)
+        normalise(NT - 4, ["s"])
+        e_quantise(NT - 3)
+        e_evacuate_regrouped(NT - 2, ["v"])
+        weighted_sum(NT - 3, 1)
+        normalise(NT - 3, ["s"])
+        store(NT - 4, 2)
+        e_quantise(NT - 2)
+        weighted_sum(NT - 2, 1)
+        e_evacuate_regrouped(NT - 1, ["v", "s"])
+        e_quantise(NT - 1)
+        weighted_sum(NT - 1, 2)
+        normalise(NT - 2, ["s"])
+        store(NT - 2, 1)
+        normalise(NT - 1, ["v", "s"])
+        store(NT - 1, 1)

@@ -187,15 +187,16 @@ def tile_attention_prop_pb_t_kernel(tc, A, qe1, ke1, ve1, out):
 
         def exponent(i):
             e_sb[i] = work.tile([P, NK], BF16, name="e")
-            rs[i] = small.tile([P, 1], F32, name="rs")
+            if i % 2 == 0:
+                rs[i // 2] = small.tile([P, 2], F32, name="rs")
             nc.scalar.activation(out=e_sb[i][:], in_=m_sb[i][:], func=ACT.Exp, bias=nmx[i][:, 0:1], scale=-1.0,
-                                 accum_out=rs[i][:, 0:1])
+                                 accum_out=rs[i // 2][:, i % 2:i % 2 + 1])
 
         def e_transpose(i, banks):
             per = 8 // banks
             et_ps[i] = [ps_et.tile([P, per, P], BF16, name="et")]
             if banks == 2:
-                et_ps[i].append(ps_s.tile([P, per, P], BF16, name="et_s", tag="s"))
+                et_ps[i].append(ps_qt.tile([P, per, P], BF16, name="et_q", tag="qt"))
             for j in range(8):
                 nc.tensor.transpose(et_ps[i][j // per][:, j % per, :], e_sb[i][:, P * j:P * j + P], ident_b[:])
 
@@ -214,14 +215,14 @@ def tile_attention_prop_pb_t_kernel(tc, A, qe1, ke1, ve1, out):
             )
 
         def e_regroup_on_vector(i):
-            eg[i] = work.tile([P, NK], BF16, name="eg", align_bytes=64, bufs=1)
+            eg[i] = keep.tile([P, NK], BF16, name="eg_tail%d" % i, align_bytes=64)
             nc.vector.tensor_copy(
                 out=eg[i][:].rearrange("p (g q t) -> p g q t", g=2, t=4),
                 in_=ex[i][:].rearrange("p (g t) q -> p g q t", t=4),
             )
 
         def e_evacuate_regrouped(i, engines):
-            eg[i] = work.tile([P, NK], BF16, name="eg", align_bytes=64, bufs=1)
+            eg[i] = keep.tile([P, NK], BF16, name="eg_tail%d" % i, align_bytes=64)
             dst = eg[i][:].rearrange("p (g q t) -> p g q t", g=2, t=4)
             if len(engines) == 1:
                 copy_on(engines[0], dst, et_ps[i][0][:].rearrange("p (g t) q -> p g q t", t=4))
@@ -233,15 +234,16 @@ def tile_attention_prop_pb_t_kernel(tc, A, qe1, ke1, ve1, out):
             ec[i] = work.tile([P, 2 * P], U32, name="ec", align_bytes=64)
             es[i] = work.tile([P, 2 * P], U8, name="es", align_bytes=64)
             nc.vector.quantize_mx(out=ec[i][:].bitcast(FP8X4), scales=es[i][:], in_=eg[i][:])
-            rr[i] = small.tile([P, 1], F32, name="rr")
-            nc.vector.reciprocal(out=rr[i][:], in_=rs[i][:])
+            if i % 2 == 0:
+                rr[i // 2] = small.tile([P, 2], F32, name="rr")
+                nc.vector.reciprocal(out=rr[i // 2][:], in_=rs[i // 2][:])
 
-        def weighted_sum(i, banks):
+        def weighted_sum(i, banks, borrow=False):
             width = F // banks
-            if banks == 1:
-                o_ps[i] = [ps_o.tile([P, F], F32, name="o")]
+            if borrow:
+                o_ps[i] = [ps_s.tile([P, width], F32, name="o_s", tag="s") for h in range(banks)]
             else:
-                o_ps[i] = [ps_s.tile([P, width], F32, name="o_half", tag="s") for h in range(banks)]
+                o_ps[i] = [ps_o.tile([P, F], F32, name="o")]
             for h in range(banks):
                 for g in range(2):
                     c0 = 512 * g + width * h
@@ -262,12 +264,15 @@ def tile_attention_prop_pb_t_kernel(tc, A, qe1, ke1, ve1, out):
             for h in range(len(engines)):
                 dst = o_sb[i // 2][:, i % 2, width * h:width * h + width]
                 if engines[h] == "v":
-                    nc.vector.tensor_scalar(out=dst, in0=o_ps[i][h][:], scalar1=rr[i][:, 0:1], scalar2=None, op0=ALU.mult)
+                    nc.vector.tensor_scalar(out=dst, in0=o_ps[i][h][:], scalar1=rr[i // 2][:, i % 2:i % 2 + 1], scalar2=None, op0=ALU.mult)
                 else:
-                    nc.scalar.activation(out=dst, in_=o_ps[i][h][:], func=ACT.Copy, scale=rr[i][:, 0:1])
+                    nc.scalar.activation(out=dst, in_=o_ps[i][h][:], func=ACT.Copy, scale=rr[i // 2][:, i % 2:i % 2 + 1])
 
         def store(first, count):
             nc.sync.dma_start(out=o_view[:, first:first + count, :], in_=o_sb[first // 2][:, first % 2:first % 2 + count, :])
+
+        def store_half(i, h):
+            nc.sync.dma_start(out=o_view[:, i, 256 * h:256 * h + 256], in_=o_sb[i // 2][:, i % 2, 256 * h:256 * h + 256])
 
         k_transpose(0)
         k_transpose(1)
@@ -276,21 +281,20 @@ def tile_attention_prop_pb_t_kernel(tc, A, qe1, ke1, ve1, out):
         k_evacuate(1, "v")
         q_evacuate(0, "s")
         k_quantise(0)
-        k_transpose(2)
-        k_evacuate(2, "v")
         k_quantise(1)
         q_quantise(0)
+        k_transpose(2)
         k_transpose(3)
         q_transpose(1)
         scores(0, 0)
-        k_evacuate(3, "s")
-        q_evacuate(1, "s")
+        k_evacuate(2, "s")
+        k_evacuate(3, "v")
         k_quantise(2)
         k_quantise(3)
+        q_evacuate(1, "s")
         scores(0, 1)
         scores(1, 0)
         v_regroup(0, 0, "s")
-        q_transpose(2, borrow=True)
 
         def live(x):
             return 0 <= x < NT
@@ -319,6 +323,8 @@ def tile_attention_prop_pb_t_kernel(tc, A, qe1, ke1, ve1, out):
                 scores(i + 2, 0)
             if live(i - 1):
                 e_transpose(i - 1, 1)
+            if i == 0:
+                q_transpose(2, borrow=True)
             if i % 2 == 0 and (i + 6) // 2 < NPAIR:
                 q_transpose((i + 6) // 2)
             if live(i - 4):
@@ -337,22 +343,23 @@ def tile_attention_prop_pb_t_kernel(tc, A, qe1, ke1, ve1, out):
             if i % 2 == 0 and (i + 6) // 2 < NPAIR:
                 q_evacuate((i + 6) // 2, "s")
 
-        e_quantise(NT - 4)
-        e_regroup_on_vector(NT - 3)
-        weighted_sum(NT - 4, 1)
-        e_transpose(NT - 1, 2)
-        normalise(NT - 4, ["s"])
-        e_quantise(NT - 3)
         e_evacuate_regrouped(NT - 2, ["v"])
+        e_transpose(NT - 1, 2)
+        e_quantise(NT - 4)
+        weighted_sum(NT - 4, 1)
+        e_regroup_on_vector(NT - 3)
+        e_quantise(NT - 3)
         weighted_sum(NT - 3, 1)
-        normalise(NT - 3, ["s"])
-        store(NT - 4, 2)
         e_quantise(NT - 2)
-        weighted_sum(NT - 2, 1)
+        weighted_sum(NT - 2, 1, borrow=True)
         e_evacuate_regrouped(NT - 1, ["v", "s"])
         e_quantise(NT - 1)
-        weighted_sum(NT - 1, 2)
-        normalise(NT - 2, ["s"])
+        weighted_sum(NT - 1, 2, borrow=True)
+        normalise(NT - 4, ["s"])
+        normalise(NT - 3, ["s"])
+        store(NT - 4, 2)
+        normalise(NT - 2, ["v"])
         store(NT - 2, 1)
         normalise(NT - 1, ["v", "s"])
-        store(NT - 1, 1)
+        store_half(NT - 1, 0)
+        store_half(NT - 1, 1)

@@ -38,8 +38,6 @@ def tile_attention_prop_pb_t_kernel(tc, A, qe1, ke1, ve1, out):
 
         ident_f = keep.tile([P, P], F32, name="ident_f")
         make_identity(nc, ident_f[:])
-        ident_b = keep.tile([P, P], BF16, name="ident_b")
-        make_identity(nc, ident_b[:])
         warm = keep.tile([P, 1], F32, name="warm")
         nc.vector.memset(warm[:], 0.0)
         warm2 = keep.tile([P, 1], F32, name="warm2")
@@ -53,7 +51,7 @@ def tile_attention_prop_pb_t_kernel(tc, A, qe1, ke1, ve1, out):
         k_sb = keep.tile([P, 8, F], BF16, name="k_sb")
         v_sb = keep.tile([P, 8, F], BF16, name="v_sb")
         k_view = ke1.rearrange("(j p) f -> p j f", p=P)
-        v_view = ve1.rearrange("(j p) f -> p j f", p=P)
+        v_view = ve1.rearrange("(j p e) f -> p j e f", p=P, e=2)
 
         def load_q(c):
             nc.sync.dma_start(out=q_sb[c][:], in_=q_view[:, 2 * c:2 * c + 2, :])
@@ -71,7 +69,7 @@ def tile_attention_prop_pb_t_kernel(tc, A, qe1, ke1, ve1, out):
         load_k(3)
         nc.sync.dma_start(out=a_sb[0][:, 0, :], in_=a_view[:, 0, :])
         load_q(1)
-        nc.sync.dma_start(out=v_sb[:], in_=v_view)
+        nc.sync.dma_start(out=v_sb[:].rearrange("p (j e) f -> p j e f", e=2), in_=v_view)
         nc.sync.dma_start(out=a_sb[0][:, 1, :], in_=a_view[:, 1, :])
         load_q(2)
         for c in range(1, NPAIR):
@@ -193,50 +191,31 @@ def tile_attention_prop_pb_t_kernel(tc, A, qe1, ke1, ve1, out):
                                  accum_out=rs[i // 2][:, i % 2:i % 2 + 1])
 
         def e_transpose(i, banks):
-            per = 8 // banks
-            et_ps[i] = [ps_et.tile([P, per, P], BF16, name="et")]
+            per = 4 // banks
+            et_ps[i] = [ps_et.tile([P, per, P], F32, name="et")]
             if banks == 2:
-                et_ps[i].append(ps_qt.tile([P, per, P], BF16, name="et_q", tag="qt"))
-            for j in range(8):
-                nc.tensor.transpose(et_ps[i][j // per][:, j % per, :], e_sb[i][:, P * j:P * j + P], ident_b[:])
+                et_ps[i].append(ps_qt.tile([P, per, P], F32, name="et_q", tag="qt"))
+            words = e_sb[i][:].bitcast(F32)
+            for w in range(4):
+                nc.tensor.transpose(et_ps[i][w // per][:, w % per, :], words[:, P * w:P * w + P], ident_f[:])
 
-        def e_evacuate(i):
-            ex[i] = work.tile([P, 8, P], BF16, name="ex")
-            nc.scalar.copy(out=ex[i][:], in_=et_ps[i][0][:])
-
-        def e_regroup(i):
-            eg[i] = work.tile([P, NK], BF16, name="eg", align_bytes=64, bufs=1)
-            if i == 0:
-                nc.vector.memset(eg[i][:, 0:2], 0.0)
-            nc.gpsimd.tensor_scalar(
-                out=eg[i][:].rearrange("p (g q t) -> p g q t", g=2, t=4),
-                in0=ex[i][:].rearrange("p (g t) q -> p g q t", t=4),
-                scalar1=1.0, scalar2=0.0, op0=ALU.mult, op1=ALU.add,
-            )
-
-        def e_regroup_on_vector(i):
-            eg[i] = keep.tile([P, NK], BF16, name="eg_tail%d" % i, align_bytes=64)
-            nc.vector.tensor_copy(
-                out=eg[i][:].rearrange("p (g q t) -> p g q t", g=2, t=4),
-                in_=ex[i][:].rearrange("p (g t) q -> p g q t", t=4),
-            )
-
-        def e_evacuate_regrouped(i, engines):
-            eg[i] = keep.tile([P, NK], BF16, name="eg_tail%d" % i, align_bytes=64)
-            dst = eg[i][:].rearrange("p (g q t) -> p g q t", g=2, t=4)
+        def e_evacuate(i, engines):
+            eg[i] = work.tile([P, NK], BF16, name="eg", align_bytes=64)
+            dst = eg[i][:].bitcast(F32).rearrange("p (g q u) -> p g q u", g=2, u=2)
             if len(engines) == 1:
-                copy_on(engines[0], dst, et_ps[i][0][:].rearrange("p (g t) q -> p g q t", t=4))
+                copy_on(engines[0], dst, et_ps[i][0][:].rearrange("p (g u) q -> p g q u", u=2))
             else:
                 for g in range(2):
-                    copy_on(engines[g], dst[:, g], et_ps[i][g][:].rearrange("p t q -> p q t"))
+                    copy_on(engines[g], dst[:, g], et_ps[i][g][:].rearrange("p u q -> p q u"))
 
         def e_quantise(i):
             ec[i] = work.tile([P, 2 * P], U32, name="ec", align_bytes=64)
             es[i] = work.tile([P, 2 * P], U8, name="es", align_bytes=64)
             nc.vector.quantize_mx(out=ec[i][:].bitcast(FP8X4), scales=es[i][:], in_=eg[i][:])
-            if i % 2 == 0:
-                rr[i // 2] = small.tile([P, 2], F32, name="rr")
-                nc.vector.reciprocal(out=rr[i // 2][:], in_=rs[i // 2][:])
+
+        def invert_sums(j):
+            rr[j] = small.tile([P, 2], F32, name="rr")
+            nc.vector.reciprocal(out=rr[j][:], in_=rs[j][:])
 
         def weighted_sum(i, banks, borrow=False):
             width = F // banks
@@ -309,57 +288,48 @@ def tile_attention_prop_pb_t_kernel(tc, A, qe1, ke1, ve1, out):
             if live(i + 1):
                 scores(i + 1, 1)
             mask(i, 1)
-            if i == 2:
-                q_quantise(2)
-            if i % 2 == 1 and i > 1 and (i + 3) // 2 < NPAIR:
+            if i % 2 == 1 and (i + 3) // 2 < NPAIR:
                 q_quantise((i + 3) // 2)
-            if i == 2 or i == 3:
-                v_quantise(i - 2)
-            if live(i - 4):
-                e_quantise(i - 4)
-            if live(i - 3):
-                e_regroup(i - 3)
+            if i == 2:
+                v_quantise(0)
+                v_quantise(1)
+            if live(i - 2):
+                e_quantise(i - 2)
             if live(i + 2):
                 scores(i + 2, 0)
             if live(i - 1):
                 e_transpose(i - 1, 1)
             if i == 0:
                 q_transpose(2, borrow=True)
-            if i % 2 == 0 and (i + 6) // 2 < NPAIR:
-                q_transpose((i + 6) // 2)
-            if live(i - 4):
-                weighted_sum(i - 4, 1)
+            if i % 2 == 1 and (i + 5) // 2 < NPAIR:
+                q_transpose((i + 5) // 2)
+            if live(i - 2):
+                weighted_sum(i - 2, 1)
             row_max(i)
+            if i % 2 == 0 and i > 0:
+                invert_sums((i - 2) // 2)
+            if live(i - 1):
+                e_evacuate(i - 1, ["s"])
+            if i % 2 == 1 and (i + 5) // 2 < NPAIR:
+                q_evacuate((i + 5) // 2, "s")
             exponent(i)
             if i == 0:
                 q_evacuate(2, "s")
                 v_regroup(0, 1, "s")
-            if live(i - 1) and i - 1 < NT - 2:
-                e_evacuate(i - 1)
-            if live(i - 4):
-                normalise(i - 4, ["s"])
-                if (i - 4) % 2 == 1:
-                    store(i - 5, 2)
-            if i % 2 == 0 and (i + 6) // 2 < NPAIR:
-                q_evacuate((i + 6) // 2, "s")
+            if live(i - 2):
+                normalise(i - 2, ["s"])
+                if (i - 2) % 2 == 1:
+                    store(i - 3, 2)
 
-        e_evacuate_regrouped(NT - 2, ["v"])
-        e_transpose(NT - 1, 2)
-        e_quantise(NT - 4)
-        weighted_sum(NT - 4, 1)
-        e_regroup_on_vector(NT - 3)
-        e_quantise(NT - 3)
-        weighted_sum(NT - 3, 1)
         e_quantise(NT - 2)
-        weighted_sum(NT - 2, 1, borrow=True)
-        e_evacuate_regrouped(NT - 1, ["v", "s"])
-        e_quantise(NT - 1)
-        weighted_sum(NT - 1, 2, borrow=True)
-        normalise(NT - 4, ["s"])
-        normalise(NT - 3, ["s"])
-        store(NT - 4, 2)
+        weighted_sum(NT - 2, 1)
+        e_transpose(NT - 1, 2)
+        invert_sums(NPAIR - 1)
         normalise(NT - 2, ["v"])
         store(NT - 2, 1)
+        e_evacuate(NT - 1, ["v", "s"])
+        e_quantise(NT - 1)
+        weighted_sum(NT - 1, 2, borrow=True)
         normalise(NT - 1, ["v", "s"])
         store_half(NT - 1, 0)
         store_half(NT - 1, 1)

@@ -290,11 +290,10 @@ def tile_attention_prop_pb_t_kernel(tc, A, qe1, ke1, ve1, out):
             mask(i, 1)
             if i % 2 == 1 and (i + 3) // 2 < NPAIR:
                 q_quantise((i + 3) // 2)
-            if i == 2:
-                v_quantise(0)
-                v_quantise(1)
-            if live(i - 2):
-                e_quantise(i - 2)
+            if i == 2 or i == 3:
+                v_quantise(i - 2)
+            if live(i - 3):
+                e_quantise(i - 3)
             if live(i + 2):
                 scores(i + 2, 0)
             if live(i - 1):
@@ -303,33 +302,37 @@ def tile_attention_prop_pb_t_kernel(tc, A, qe1, ke1, ve1, out):
                 q_transpose(2, borrow=True)
             if i % 2 == 1 and (i + 5) // 2 < NPAIR:
                 q_transpose((i + 5) // 2)
-            if live(i - 2):
-                weighted_sum(i - 2, 1)
+            if live(i - 3):
+                weighted_sum(i - 3, 1)
             row_max(i)
-            if i % 2 == 0 and i > 0:
-                invert_sums((i - 2) // 2)
-            if live(i - 1):
-                e_evacuate(i - 1, ["s"])
-            if i % 2 == 1 and (i + 5) // 2 < NPAIR:
-                q_evacuate((i + 5) // 2, "s")
+            if i % 2 == 1 and i > 1:
+                invert_sums((i - 3) // 2)
             exponent(i)
             if i == 0:
                 q_evacuate(2, "s")
                 v_regroup(0, 1, "s")
-            if live(i - 2):
-                normalise(i - 2, ["s"])
-                if (i - 2) % 2 == 1:
-                    store(i - 3, 2)
+            if live(i - 1):
+                e_evacuate(i - 1, ["s"])
+            if live(i - 3):
+                normalise(i - 3, ["s"])
+                if (i - 3) % 2 == 1:
+                    store(i - 4, 2)
+            if i % 2 == 1 and (i + 5) // 2 < NPAIR:
+                q_evacuate((i + 5) // 2, "s")
 
+        e_quantise(NT - 3)
+        weighted_sum(NT - 3, 1)
+        e_transpose(NT - 1, 2)
+        normalise(NT - 3, ["v"])
+        store(NT - 4, 2)
         e_quantise(NT - 2)
         weighted_sum(NT - 2, 1)
-        e_transpose(NT - 1, 2)
         invert_sums(NPAIR - 1)
-        normalise(NT - 2, ["v"])
-        store(NT - 2, 1)
         e_evacuate(NT - 1, ["v", "s"])
         e_quantise(NT - 1)
         weighted_sum(NT - 1, 2, borrow=True)
+        normalise(NT - 2, ["v"])
+        store(NT - 2, 1)
         normalise(NT - 1, ["v", "s"])
         store_half(NT - 1, 0)
         store_half(NT - 1, 1)

@@ -68,12 +68,13 @@ def tile_attention_prop_pb_t_kernel(tc, A, qe1, ke1, ve1, out):
         load_k(2)
         load_k(3)
         nc.sync.dma_start(out=a_sb[0][:, 0, :], in_=a_view[:, 0, :])
-        load_q(1)
-        nc.sync.dma_start(out=v_sb[:].rearrange("p (j e) f -> p j e f", e=2), in_=v_view)
         nc.sync.dma_start(out=a_sb[0][:, 1, :], in_=a_view[:, 1, :])
+        load_q(1)
         load_q(2)
         for c in range(1, NPAIR):
             load_a(c)
+            if c == 1:
+                nc.sync.dma_start(out=v_sb[:].rearrange("p (j e) f -> p j e f", e=2), in_=v_view)
             if c + 2 < NPAIR:
                 load_q(c + 2)
 
@@ -169,7 +170,7 @@ def tile_attention_prop_pb_t_kernel(tc, A, qe1, ke1, ve1, out):
 
         def mask(i, g):
             if g == 0:
-                m_sb[i] = work.tile([P, NK], F32, name="m")
+                m_sb[i] = work.tile([P, NK], F32, name="m", bufs=4)
             nc.vector.scalar_tensor_tensor(
                 out=m_sb[i][:, 512 * g:512 * g + 512],
                 in0=s_ps[(i, g)][:],
@@ -189,6 +190,18 @@ def tile_attention_prop_pb_t_kernel(tc, A, qe1, ke1, ve1, out):
                 rs[i // 2] = small.tile([P, 2], F32, name="rs")
             nc.scalar.activation(out=e_sb[i][:], in_=m_sb[i][:], func=ACT.Exp, bias=nmx[i][:, 0:1], scale=-1.0,
                                  accum_out=rs[i // 2][:, i % 2:i % 2 + 1])
+
+        def exponent_in_halves(i):
+            e_sb[i] = work.tile([P, NK], BF16, name="e")
+            halves = small.tile([P, 2], F32, name="rs_halves")
+            for g in range(2):
+                cols = slice(512 * g, 512 * g + 512)
+                nc.scalar.activation(out=e_sb[i][:, cols], in_=m_sb[i][:, cols], func=ACT.Exp, bias=nmx[i][:, 0:1], scale=-1.0,
+                                     accum_out=halves[:, g:g + 1])
+            return halves
+
+        def join_halves(i, halves):
+            nc.vector.tensor_tensor(out=rs[i // 2][:, i % 2:i % 2 + 1], in0=halves[:, 0:1], in1=halves[:, 1:2], op=ALU.add)
 
         def e_transpose(i, banks):
             per = 4 // banks
@@ -253,6 +266,9 @@ def tile_attention_prop_pb_t_kernel(tc, A, qe1, ke1, ve1, out):
         def store_half(i, h):
             nc.sync.dma_start(out=o_view[:, i, 256 * h:256 * h + 256], in_=o_sb[i // 2][:, i % 2, 256 * h:256 * h + 256])
 
+        def live(x):
+            return 0 <= x < NT
+
         k_transpose(0)
         k_transpose(1)
         q_transpose(0)
@@ -264,73 +280,87 @@ def tile_attention_prop_pb_t_kernel(tc, A, qe1, ke1, ve1, out):
         q_quantise(0)
         k_transpose(2)
         k_transpose(3)
-        q_transpose(1)
         scores(0, 0)
         k_evacuate(2, "s")
-        k_evacuate(3, "v")
+        k_evacuate(3, "s")
         k_quantise(2)
         k_quantise(3)
-        q_evacuate(1, "s")
-        scores(0, 1)
         scores(1, 0)
-        v_regroup(0, 0, "s")
+        q_transpose(1)
+        scores(0, 1)
+        mask(0, 0)
+        mask(1, 0)
+        q_evacuate(1, "s")
+        scores(1, 1)
+        mask(0, 1)
+        q_quantise(1)
+        scores(2, 0)
+        scores(2, 1)
+        q_transpose(2, borrow=True)
+        q_evacuate(2, "s")
 
-        def live(x):
-            return 0 <= x < NT
-
-        for i in range(NT):
-            mask(i, 0)
-            if i == 0:
-                q_quantise(1)
+        for i in range(1, NT):
+            odd = i % 2 == 1
+            if not odd and (i + 2) // 2 < NPAIR:
+                q_quantise((i + 2) // 2)
+            if i == 2:
                 nc.vector.memset(vg[:, 2048:2050], 0.0)
                 v_regroup(1, 0, "g")
                 v_regroup(1, 1, "g")
-            if live(i + 1):
-                scores(i + 1, 1)
+            if i == 3 or i == 4:
+                v_quantise(4 - i)
+            if live(i - 4):
+                e_quantise(i - 4)
+                weighted_sum(i - 4, 1)
             mask(i, 1)
-            if i % 2 == 1 and (i + 3) // 2 < NPAIR:
-                q_quantise((i + 3) // 2)
-            if i == 2 or i == 3:
-                v_quantise(i - 2)
-            if live(i - 3):
-                e_quantise(i - 3)
+            if live(i - 2):
+                e_transpose(i - 2, 1)
+            if odd and (i + 5) // 2 < NPAIR:
+                q_transpose((i + 5) // 2)
             if live(i + 2):
                 scores(i + 2, 0)
-            if live(i - 1):
-                e_transpose(i - 1, 1)
-            if i == 0:
-                q_transpose(2, borrow=True)
-            if i % 2 == 1 and (i + 5) // 2 < NPAIR:
-                q_transpose((i + 5) // 2)
-            if live(i - 3):
-                weighted_sum(i - 3, 1)
-            row_max(i)
-            if i % 2 == 1 and i > 1:
-                invert_sums((i - 3) // 2)
-            exponent(i)
-            if i == 0:
-                q_evacuate(2, "s")
-                v_regroup(0, 1, "s")
-            if live(i - 1):
-                e_evacuate(i - 1, ["s"])
-            if live(i - 3):
-                normalise(i - 3, ["s"])
-                if (i - 3) % 2 == 1:
-                    store(i - 4, 2)
-            if i % 2 == 1 and (i + 5) // 2 < NPAIR:
+            row_max(i - 1)
+            if live(i - 4) and not odd:
+                invert_sums((i - 4) // 2)
+            if live(i + 1):
+                mask(i + 1, 0)
+            if live(i + 2):
+                scores(i + 2, 1)
+            exponent(i - 1)
+            if i == 1 or i == 2:
+                v_regroup(0, i - 1, "s")
+            if live(i - 2) and i < NT - 1:
+                e_evacuate(i - 2, ["s"])
+            if live(i - 4) and i < NT - 1:
+                normalise(i - 4, ["s"])
+                if (i - 4) % 2 == 1:
+                    store(i - 5, 2)
+            if odd and (i + 5) // 2 < NPAIR:
                 q_evacuate((i + 5) // 2, "s")
 
+        row_max(NT - 1)
+        halves = exponent_in_halves(NT - 1)
+        e_quantise(NT - 4)
+        e_transpose(NT - 2, 1)
+        weighted_sum(NT - 4, 1)
+        e_evacuate(NT - 3, ["v"])
+        normalise(NT - 5, ["s"])
+        store(NT - 6, 2)
+        invert_sums(NPAIR - 2)
         e_quantise(NT - 3)
-        weighted_sum(NT - 3, 1)
         e_transpose(NT - 1, 2)
-        normalise(NT - 3, ["v"])
-        store(NT - 4, 2)
+        weighted_sum(NT - 3, 1)
+        e_evacuate(NT - 2, ["v"])
+        e_evacuate(NT - 1, ["s", "v"])
         e_quantise(NT - 2)
-        weighted_sum(NT - 2, 1)
-        invert_sums(NPAIR - 1)
-        e_evacuate(NT - 1, ["v", "s"])
+        weighted_sum(NT - 2, 1, borrow=True)
+        normalise(NT - 4, ["s"])
         e_quantise(NT - 1)
         weighted_sum(NT - 1, 2, borrow=True)
+        join_halves(NT - 1, halves)
+        normalise(NT - 3, ["s"])
+        store(NT - 4, 2)
+        invert_sums(NPAIR - 1)
         normalise(NT - 2, ["v"])
         store(NT - 2, 1)
         normalise(NT - 1, ["v", "s"])

@@ -17,6 +17,7 @@ P = 128
 NQ, NK, F = 4096, 1024, 512
 NT = NQ // P
 NPAIR = NT // 2
+W = 160
 FLOPS = 2 * NQ * NK * F * 2
 PIN = True
 
@@ -68,13 +69,12 @@ def tile_attention_prop_pb_t_kernel(tc, A, qe1, ke1, ve1, out):
         load_k(2)
         load_k(3)
         nc.sync.dma_start(out=a_sb[0][:, 0, :], in_=a_view[:, 0, :])
-        nc.sync.dma_start(out=a_sb[0][:, 1, :], in_=a_view[:, 1, :])
         load_q(1)
+        nc.sync.dma_start(out=a_sb[0][:, 1, :], in_=a_view[:, 1, :])
         load_q(2)
+        nc.sync.dma_start(out=v_sb[:].rearrange("p (j e) f -> p j e f", e=2), in_=v_view)
         for c in range(1, NPAIR):
             load_a(c)
-            if c == 1:
-                nc.sync.dma_start(out=v_sb[:].rearrange("p (j e) f -> p j e f", e=2), in_=v_view)
             if c + 2 < NPAIR:
                 load_q(c + 2)
 
@@ -170,9 +170,9 @@ def tile_attention_prop_pb_t_kernel(tc, A, qe1, ke1, ve1, out):
 
         def mask(i, g):
             if g == 0:
-                m_sb[i] = work.tile([P, NK], F32, name="m", bufs=4)
+                m_sb[i] = work.tile([P, W + NK], F32, name="m", bufs=4)
             nc.vector.scalar_tensor_tensor(
-                out=m_sb[i][:, 512 * g:512 * g + 512],
+                out=m_sb[i][:, W + 512 * g:W + 512 * g + 512],
                 in0=s_ps[(i, g)][:],
                 scalar=-inv_sqrt_f,
                 in1=a_sb[i // 2][:, i % 2, 512 * g:512 * g + 512],
@@ -180,15 +180,26 @@ def tile_attention_prop_pb_t_kernel(tc, A, qe1, ke1, ve1, out):
                 op1=ALU.mult,
             )
 
+        def paired(i):
+            return 3 <= i < NT - 1
+
+        def pair_min(i):
+            a = m_sb[i][:, NK - W:NK]
+            b = m_sb[i][:, NK:NK + W]
+            d = small.tile([P, W], F32, name="d", bufs=2)
+            nc.gpsimd.tensor_tensor(out=d[:], in0=a, in1=b, op=ALU.subtract)
+            nc.gpsimd.tensor_scalar(out=d[:], in0=d[:], scalar1=0.0, scalar2=-3.0e38, op0=ALU.min, op1=ALU.max)
+            nc.gpsimd.tensor_tensor(out=m_sb[i][:, 0:W], in0=b, in1=d[:], op=ALU.add)
+
         def row_max(i):
             nmx[i] = small.tile([P, 1], F32, name="nmx")
-            nc.vector.tensor_reduce(out=nmx[i][:], in_=m_sb[i][:], axis=AX.X, op=ALU.min)
+            nc.vector.tensor_reduce(out=nmx[i][:], in_=m_sb[i][:, 0:NK - W] if paired(i) else m_sb[i][:, W:W + NK], axis=AX.X, op=ALU.min)
 
         def exponent(i):
             e_sb[i] = work.tile([P, NK], BF16, name="e")
             if i % 2 == 0:
                 rs[i // 2] = small.tile([P, 2], F32, name="rs")
-            nc.scalar.activation(out=e_sb[i][:], in_=m_sb[i][:], func=ACT.Exp, bias=nmx[i][:, 0:1], scale=-1.0,
+            nc.scalar.activation(out=e_sb[i][:], in_=m_sb[i][:, W:W + NK], func=ACT.Exp, bias=nmx[i][:, 0:1], scale=-1.0,
                                  accum_out=rs[i // 2][:, i % 2:i % 2 + 1])
 
         def exponent_in_halves(i):
@@ -196,7 +207,7 @@ def tile_attention_prop_pb_t_kernel(tc, A, qe1, ke1, ve1, out):
             halves = small.tile([P, 2], F32, name="rs_halves")
             for g in range(2):
                 cols = slice(512 * g, 512 * g + 512)
-                nc.scalar.activation(out=e_sb[i][:, cols], in_=m_sb[i][:, cols], func=ACT.Exp, bias=nmx[i][:, 0:1], scale=-1.0,
+                nc.scalar.activation(out=e_sb[i][:, cols], in_=m_sb[i][:, W + 512 * g:W + 512 * g + 512], func=ACT.Exp, bias=nmx[i][:, 0:1], scale=-1.0,
                                      accum_out=halves[:, g:g + 1])
             return halves
 
@@ -282,28 +293,28 @@ def tile_attention_prop_pb_t_kernel(tc, A, qe1, ke1, ve1, out):
         k_transpose(3)
         scores(0, 0)
         k_evacuate(2, "s")
-        k_evacuate(3, "s")
+        k_evacuate(3, "v")
         k_quantise(2)
         k_quantise(3)
         scores(1, 0)
         q_transpose(1)
-        scores(0, 1)
         mask(0, 0)
+        scores(0, 1)
         mask(1, 0)
         q_evacuate(1, "s")
-        scores(1, 1)
-        mask(0, 1)
-        q_quantise(1)
-        scores(2, 0)
-        scores(2, 1)
-        q_transpose(2, borrow=True)
-        q_evacuate(2, "s")
 
-        for i in range(1, NT):
+        for i in range(NT):
             odd = i % 2 == 1
-            if not odd and (i + 2) // 2 < NPAIR:
-                q_quantise((i + 2) // 2)
-            if i == 2:
+            if i > 1:
+                mask(i, 0)
+            if live(i + 1):
+                scores(i + 1, 1)
+            mask(i, 1)
+            if i == 0:
+                q_quantise(1)
+            if odd and (i + 3) // 2 < NPAIR:
+                q_quantise((i + 3) // 2)
+            if i == 1:
                 nc.vector.memset(vg[:, 2048:2050], 0.0)
                 v_regroup(1, 0, "g")
                 v_regroup(1, 1, "g")
@@ -311,24 +322,28 @@ def tile_attention_prop_pb_t_kernel(tc, A, qe1, ke1, ve1, out):
                 v_quantise(4 - i)
             if live(i - 4):
                 e_quantise(i - 4)
-                weighted_sum(i - 4, 1)
-            mask(i, 1)
-            if live(i - 2):
-                e_transpose(i - 2, 1)
-            if odd and (i + 5) // 2 < NPAIR:
-                q_transpose((i + 5) // 2)
+            if paired(i):
+                pair_min(i)
             if live(i + 2):
                 scores(i + 2, 0)
-            row_max(i - 1)
+            if live(i - 2):
+                e_transpose(i - 2, 1)
+            if i == 0:
+                q_transpose(2, borrow=True)
+                q_evacuate(2, "s")
+            if odd and (i + 5) // 2 < NPAIR:
+                q_transpose((i + 5) // 2)
+            if live(i - 4):
+                weighted_sum(i - 4, 1)
+            for t in [i] if i < 2 else [i - 1] if i > 2 else []:
+                row_max(t)
+                exponent(t)
+            if i == 0:
+                v_regroup(0, 0, "s")
+            if i == 2:
+                v_regroup(0, 1, "s")
             if live(i - 4) and not odd:
                 invert_sums((i - 4) // 2)
-            if live(i + 1):
-                mask(i + 1, 0)
-            if live(i + 2):
-                scores(i + 2, 1)
-            exponent(i - 1)
-            if i == 1 or i == 2:
-                v_regroup(0, i - 1, "s")
             if live(i - 2) and i < NT - 1:
                 e_evacuate(i - 2, ["s"])
             if live(i - 4) and i < NT - 1:

@@ -17,7 +17,7 @@ P = 128
 NQ, NK, F = 4096, 1024, 512
 NT = NQ // P
 NPAIR = NT // 2
-W = 160
+W = 192
 FLOPS = 2 * NQ * NK * F * 2
 PIN = True
 
@@ -44,6 +44,9 @@ def tile_attention_prop_pb_t_kernel(tc, A, qe1, ke1, ve1, out):
         warm2 = keep.tile([P, 1], F32, name="warm2")
         nc.scalar.activation(out=warm2[:], in_=warm[:], func=ACT.Exp)
 
+        minus_one = keep.tile([P, 2], F32, name="minus_one")
+        nc.gpsimd.memset(minus_one[:], -1.0)
+
         q_view = qe1.rearrange("(p n) f -> p n f", n=NT)
         a_view = A.rearrange("(p n) k -> p n k", n=NT)
         o_view = out.rearrange("(p n) f -> p n f", n=NT)
@@ -60,6 +63,9 @@ def tile_attention_prop_pb_t_kernel(tc, A, qe1, ke1, ve1, out):
         def load_a(c):
             nc.sync.dma_start(out=a_sb[c][:], in_=a_view[:, 2 * c:2 * c + 2, :])
 
+        def load_a_tile(i):
+            nc.sync.dma_start(out=a_sb[i // 2][:, i % 2, :], in_=a_view[:, i, :])
+
         def load_k(b):
             nc.sync.dma_start(out=k_sb[:, 2 * b:2 * b + 2, :], in_=k_view[:, 2 * b:2 * b + 2, :])
 
@@ -68,12 +74,15 @@ def tile_attention_prop_pb_t_kernel(tc, A, qe1, ke1, ve1, out):
         load_q(0)
         load_k(2)
         load_k(3)
-        nc.sync.dma_start(out=a_sb[0][:, 0, :], in_=a_view[:, 0, :])
+        load_a_tile(0)
         load_q(1)
-        nc.sync.dma_start(out=a_sb[0][:, 1, :], in_=a_view[:, 1, :])
+        load_a_tile(1)
+        load_a_tile(2)
         load_q(2)
+        load_a_tile(3)
         nc.sync.dma_start(out=v_sb[:].rearrange("p (j e) f -> p j e f", e=2), in_=v_view)
-        for c in range(1, NPAIR):
+        load_q(3)
+        for c in range(2, NPAIR):
             load_a(c)
             if c + 2 < NPAIR:
                 load_q(c + 2)
@@ -180,6 +189,14 @@ def tile_attention_prop_pb_t_kernel(tc, A, qe1, ke1, ve1, out):
                 op1=ALU.mult,
             )
 
+        def mask_off_vector(i, g):
+            if g == 0:
+                m_sb[i] = work.tile([P, W + NK], F32, name="m", bufs=4)
+            raw = small.tile([P, 512], F32, name="raw", bufs=2)
+            nc.scalar.activation(out=raw[:], in_=s_ps[(i, g)][:], func=ACT.Copy, scale=-inv_sqrt_f)
+            nc.gpsimd.tensor_tensor(out=m_sb[i][:, W + 512 * g:W + 512 * g + 512], in0=raw[:],
+                                    in1=a_sb[i // 2][:, i % 2, 512 * g:512 * g + 512], op=ALU.mult)
+
         def paired(i):
             return 3 <= i < NT - 1
 
@@ -196,14 +213,14 @@ def tile_attention_prop_pb_t_kernel(tc, A, qe1, ke1, ve1, out):
             nc.vector.tensor_reduce(out=nmx[i][:], in_=m_sb[i][:, 0:NK - W] if paired(i) else m_sb[i][:, W:W + NK], axis=AX.X, op=ALU.min)
 
         def exponent(i):
-            e_sb[i] = work.tile([P, NK], BF16, name="e")
+            e_sb[i] = work.tile([P, NK], BF16, name="e", bufs=4)
             if i % 2 == 0:
                 rs[i // 2] = small.tile([P, 2], F32, name="rs")
             nc.scalar.activation(out=e_sb[i][:], in_=m_sb[i][:, W:W + NK], func=ACT.Exp, bias=nmx[i][:, 0:1], scale=-1.0,
                                  accum_out=rs[i // 2][:, i % 2:i % 2 + 1])
 
         def exponent_in_halves(i):
-            e_sb[i] = work.tile([P, NK], BF16, name="e")
+            e_sb[i] = work.tile([P, NK], BF16, name="e", bufs=4)
             halves = small.tile([P, 2], F32, name="rs_halves")
             for g in range(2):
                 cols = slice(512 * g, 512 * g + 512)
@@ -214,32 +231,43 @@ def tile_attention_prop_pb_t_kernel(tc, A, qe1, ke1, ve1, out):
         def join_halves(i, halves):
             nc.vector.tensor_tensor(out=rs[i // 2][:, i % 2:i % 2 + 1], in0=halves[:, 0:1], in1=halves[:, 1:2], op=ALU.add)
 
-        def e_transpose(i, banks):
-            per = 4 // banks
-            et_ps[i] = [ps_et.tile([P, per, P], F32, name="et")]
-            if banks == 2:
-                et_ps[i].append(ps_qt.tile([P, per, P], F32, name="et_q", tag="qt"))
+        def e_transpose(i):
+            et_ps[i] = ps_et.tile([P, 4, P], F32, name="et")
             words = e_sb[i][:].bitcast(F32)
             for w in range(4):
-                nc.tensor.transpose(et_ps[i][w // per][:, w % per, :], words[:, P * w:P * w + P], ident_f[:])
+                nc.tensor.transpose(et_ps[i][:, w, :], words[:, P * w:P * w + P], ident_f[:])
 
-        def e_evacuate(i, engines):
-            eg[i] = work.tile([P, NK], BF16, name="eg", align_bytes=64)
-            dst = eg[i][:].bitcast(F32).rearrange("p (g q u) -> p g q u", g=2, u=2)
-            if len(engines) == 1:
-                copy_on(engines[0], dst, et_ps[i][0][:].rearrange("p (g u) q -> p g q u", u=2))
-            else:
-                for g in range(2):
-                    copy_on(engines[g], dst[:, g], et_ps[i][g][:].rearrange("p u q -> p q u"))
+        def e_evacuate(i, eng):
+            eg[i] = work.tile([P, NK], BF16, name="eg", align_bytes=64, bufs=4)
+            copy_on(eng, eg[i][:].bitcast(F32).rearrange("p (g q u) -> p g q u", g=2, u=2),
+                    et_ps[i][:].rearrange("p (g u) q -> p g q u", u=2))
 
-        def e_quantise(i):
+        def e_transpose_half(i, g):
+            pool, tag = (ps_et, "et") if g == 0 else (ps_qt, "qt")
+            et_ps[i, g] = pool.tile([P, 2, P], F32, name="et_half", tag=tag)
+            words = e_sb[i][:].bitcast(F32)
+            for u in range(2):
+                w = 2 * g + u
+                nc.tensor.transpose(et_ps[i, g][:, u, :], words[:, P * w:P * w + P], ident_f[:])
+
+        def e_evacuate_half(i, g, eng):
+            if g == 0:
+                eg[i] = work.tile([P, NK], BF16, name="eg", align_bytes=64, bufs=4)
+            copy_on(eng, eg[i][:, 512 * g:512 * g + 512].bitcast(F32).rearrange("p (q u) -> p q u", u=2),
+                    et_ps[i, g][:].rearrange("p u q -> p q u"))
+
+        def e_quantise(i, parts=1):
             ec[i] = work.tile([P, 2 * P], U32, name="ec", align_bytes=64)
             es[i] = work.tile([P, 2 * P], U8, name="es", align_bytes=64)
-            nc.vector.quantize_mx(out=ec[i][:].bitcast(FP8X4), scales=es[i][:], in_=eg[i][:])
+            width = 2 * P // parts
+            for h in range(parts):
+                cols = slice(width * h, width * h + width)
+                nc.vector.quantize_mx(out=ec[i][:, cols].bitcast(FP8X4), scales=es[i][:, cols],
+                                      in_=eg[i][:, 4 * width * h:4 * width * h + 4 * width])
 
         def invert_sums(j):
             rr[j] = small.tile([P, 2], F32, name="rr")
-            nc.vector.reciprocal(out=rr[j][:], in_=rs[j][:])
+            nc.gpsimd.tensor_tensor(out=rr[j][:], in0=rs[j][:], in1=minus_one[:], op=ALU.pow)
 
         def weighted_sum(i, banks, borrow=False):
             width = F // banks
@@ -247,8 +275,8 @@ def tile_attention_prop_pb_t_kernel(tc, A, qe1, ke1, ve1, out):
                 o_ps[i] = [ps_s.tile([P, width], F32, name="o_s", tag="s") for h in range(banks)]
             else:
                 o_ps[i] = [ps_o.tile([P, F], F32, name="o")]
-            for h in range(banks):
-                for g in range(2):
+            for g in range(2):
+                for h in range(banks):
                     c0 = 512 * g + width * h
                     nc.tensor.matmul_mx(
                         out=o_ps[i][h][:],
@@ -300,8 +328,8 @@ def tile_attention_prop_pb_t_kernel(tc, A, qe1, ke1, ve1, out):
         q_transpose(1)
         mask(0, 0)
         scores(0, 1)
-        mask(1, 0)
         q_evacuate(1, "s")
+        mask_off_vector(1, 0)
 
         for i in range(NT):
             odd = i % 2 == 1
@@ -309,13 +337,16 @@ def tile_attention_prop_pb_t_kernel(tc, A, qe1, ke1, ve1, out):
                 mask(i, 0)
             if live(i + 1):
                 scores(i + 1, 1)
-            mask(i, 1)
+            if i == 0:
+                mask_off_vector(1, 1)
+            if i != 1:
+                mask(i, 1)
             if i == 0:
                 q_quantise(1)
-            if odd and (i + 3) // 2 < NPAIR:
+            if odd and 2 < (i + 3) // 2 < NPAIR:
                 q_quantise((i + 3) // 2)
-            if i == 1:
-                nc.vector.memset(vg[:, 2048:2050], 0.0)
+            if i == 2:
+                q_quantise(2)
                 v_regroup(1, 0, "g")
                 v_regroup(1, 1, "g")
             if i == 3 or i == 4:
@@ -327,7 +358,7 @@ def tile_attention_prop_pb_t_kernel(tc, A, qe1, ke1, ve1, out):
             if live(i + 2):
                 scores(i + 2, 0)
             if live(i - 2):
-                e_transpose(i - 2, 1)
+                e_transpose(i - 2)
             if i == 0:
                 q_transpose(2, borrow=True)
                 q_evacuate(2, "s")
@@ -335,9 +366,12 @@ def tile_attention_prop_pb_t_kernel(tc, A, qe1, ke1, ve1, out):
                 q_transpose((i + 5) // 2)
             if live(i - 4):
                 weighted_sum(i - 4, 1)
-            for t in [i] if i < 2 else [i - 1] if i > 2 else []:
-                row_max(t)
-                exponent(t)
+            if i == 0:
+                row_max(0)
+                exponent(0)
+            elif i > 1:
+                row_max(i - 1)
+                exponent(i - 1)
             if i == 0:
                 v_regroup(0, 0, "s")
             if i == 2:
@@ -345,7 +379,7 @@ def tile_attention_prop_pb_t_kernel(tc, A, qe1, ke1, ve1, out):
             if live(i - 4) and not odd:
                 invert_sums((i - 4) // 2)
             if live(i - 2) and i < NT - 1:
-                e_evacuate(i - 2, ["s"])
+                e_evacuate(i - 2, "s")
             if live(i - 4) and i < NT - 1:
                 normalise(i - 4, ["s"])
                 if (i - 4) % 2 == 1:
@@ -355,28 +389,31 @@ def tile_attention_prop_pb_t_kernel(tc, A, qe1, ke1, ve1, out):
 
         row_max(NT - 1)
         halves = exponent_in_halves(NT - 1)
-        e_quantise(NT - 4)
-        e_transpose(NT - 2, 1)
-        weighted_sum(NT - 4, 1)
-        e_evacuate(NT - 3, ["v"])
         normalise(NT - 5, ["s"])
         store(NT - 6, 2)
+        e_quantise(NT - 4)
+        e_transpose(NT - 2)
+        e_evacuate(NT - 3, "v")
+        e_transpose_half(NT - 1, 0)
+        weighted_sum(NT - 4, 1)
+        e_transpose_half(NT - 1, 1)
         invert_sums(NPAIR - 2)
+        e_evacuate(NT - 2, "v")
         e_quantise(NT - 3)
-        e_transpose(NT - 1, 2)
+        e_evacuate_half(NT - 1, 0, "s")
+        e_evacuate_half(NT - 1, 1, "s")
         weighted_sum(NT - 3, 1)
-        e_evacuate(NT - 2, ["v"])
-        e_evacuate(NT - 1, ["s", "v"])
         e_quantise(NT - 2)
-        weighted_sum(NT - 2, 1, borrow=True)
-        normalise(NT - 4, ["s"])
-        e_quantise(NT - 1)
-        weighted_sum(NT - 1, 2, borrow=True)
         join_halves(NT - 1, halves)
-        normalise(NT - 3, ["s"])
-        store(NT - 4, 2)
+        weighted_sum(NT - 2, 1, borrow=True)
+        e_quantise(NT - 1, 2)
+        weighted_sum(NT - 1, 2, borrow=True)
         invert_sums(NPAIR - 1)
-        normalise(NT - 2, ["v"])
+        normalise(NT - 4, ["s"])
+        store(NT - 4, 1)
+        normalise(NT - 3, ["v"])
+        store(NT - 3, 1)
+        normalise(NT - 2, ["s"])
         store(NT - 2, 1)
         normalise(NT - 1, ["v", "s"])
         store_half(NT - 1, 0)

@@ -17,7 +17,7 @@ P = 128
 NQ, NK, F = 4096, 1024, 512
 NT = NQ // P
 NPAIR = NT // 2
-W = 192
+W = 176
 FLOPS = 2 * NQ * NK * F * 2
 PIN = True
 
@@ -43,9 +43,6 @@ def tile_attention_prop_pb_t_kernel(tc, A, qe1, ke1, ve1, out):
         nc.vector.memset(warm[:], 0.0)
         warm2 = keep.tile([P, 1], F32, name="warm2")
         nc.scalar.activation(out=warm2[:], in_=warm[:], func=ACT.Exp)
-
-        minus_one = keep.tile([P, 2], F32, name="minus_one")
-        nc.gpsimd.memset(minus_one[:], -1.0)
 
         q_view = qe1.rearrange("(p n) f -> p n f", n=NT)
         a_view = A.rearrange("(p n) k -> p n k", n=NT)
@@ -267,7 +264,7 @@ def tile_attention_prop_pb_t_kernel(tc, A, qe1, ke1, ve1, out):
 
         def invert_sums(j):
             rr[j] = small.tile([P, 2], F32, name="rr")
-            nc.gpsimd.tensor_tensor(out=rr[j][:], in0=rs[j][:], in1=minus_one[:], op=ALU.pow)
+            nc.vector.reciprocal(out=rr[j][:], in_=rs[j][:])
 
         def weighted_sum(i, banks, borrow=False):
             width = F // banks

@@ -350,6 +350,8 @@ def tile_attention_prop_pb_t_kernel(tc, A, qe1, ke1, ve1, out):
                 v_quantise(4 - i)
             if live(i - 4):
                 e_quantise(i - 4)
+                if not odd:
+                    invert_sums((i - 4) // 2)
             if paired(i):
                 pair_min(i)
             if live(i + 2):
@@ -373,8 +375,6 @@ def tile_attention_prop_pb_t_kernel(tc, A, qe1, ke1, ve1, out):
                 v_regroup(0, 0, "s")
             if i == 2:
                 v_regroup(0, 1, "s")
-            if live(i - 4) and not odd:
-                invert_sums((i - 4) // 2)
             if live(i - 2) and i < NT - 1:
                 e_evacuate(i - 2, "s")
             if live(i - 4) and i < NT - 1:

@@ -17,7 +17,7 @@ P = 128
 NQ, NK, F = 4096, 1024, 512
 NT = NQ // P
 NPAIR = NT // 2
-W = 176
+W = 160
 FLOPS = 2 * NQ * NK * F * 2
 PIN = True
 
@@ -43,6 +43,9 @@ def tile_attention_prop_pb_t_kernel(tc, A, qe1, ke1, ve1, out):
         nc.vector.memset(warm[:], 0.0)
         warm2 = keep.tile([P, 1], F32, name="warm2")
         nc.scalar.activation(out=warm2[:], in_=warm[:], func=ACT.Exp)
+
+        idle_in = keep.tile([P, F], BF16, name="idle_in")
+        nc.vector.memset(idle_in[:], 0.0)
 
         q_view = qe1.rearrange("(p n) f -> p n f", n=NT)
         a_view = A.rearrange("(p n) k -> p n k", n=NT)
@@ -305,6 +308,9 @@ def tile_attention_prop_pb_t_kernel(tc, A, qe1, ke1, ve1, out):
         def live(x):
             return 0 <= x < NT
 
+        for n in range(6):
+            idle_out = ps_o.tile([P, F], F32, name="idle_out", tag="o")
+            nc.tensor.matmul(idle_out[:], lhsT=idle_in[:, 0:P], rhs=idle_in[:], start=True, stop=True)
         k_transpose(0)
         k_transpose(1)
         q_transpose(0)

from contextlib import ExitStack
import math

import concourse.mybir as mybir
from concourse.masks import make_identity

F32 = mybir.dt.float32
BF16 = mybir.dt.bfloat16
U32 = mybir.dt.uint32
U8 = mybir.dt.uint8
FP8X4 = mybir.dt.float8_e4m3fn_x4
ALU = mybir.AluOpType
ACT = mybir.ActivationFunctionType
AX = mybir.AxisListType

P = 128
NQ, NK, F = 4096, 1024, 512
NT = NQ // P
NPAIR = NT // 2
W = 160
FLOPS = 2 * NQ * NK * F * 2
PIN = True


def tile_attention_prop_pb_t_kernel(tc, A, qe1, ke1, ve1, out):
    nc = tc.nc
    inv_sqrt_f = 1.0 / math.sqrt(F)
    with ExitStack() as ctx:
        if PIN:
            ctx.enter_context(tc.manual_schedule())
        keep = ctx.enter_context(tc.tile_pool(name="keep", bufs=1))
        work = ctx.enter_context(tc.tile_pool(name="work", bufs=3))
        small = ctx.enter_context(tc.tile_pool(name="small", bufs=8))
        outp = ctx.enter_context(tc.tile_pool(name="outp", bufs=4))
        ps_s = ctx.enter_context(tc.psum_pool(name="ps_s", bufs=3))
        ps_et = ctx.enter_context(tc.psum_pool(name="ps_et", bufs=2))
        ps_o = ctx.enter_context(tc.psum_pool(name="ps_o", bufs=2))
        ps_qt = ctx.enter_context(tc.psum_pool(name="ps_qt", bufs=1))

        ident_f = keep.tile([P, P], F32, name="ident_f")
        make_identity(nc, ident_f[:])
        warm = keep.tile([P, 1], F32, name="warm")
        nc.vector.memset(warm[:], 0.0)
        warm2 = keep.tile([P, 1], F32, name="warm2")
        nc.scalar.activation(out=warm2[:], in_=warm[:], func=ACT.Exp)

        idle_in = keep.tile([P, F], BF16, name="idle_in")
        nc.vector.memset(idle_in[:], 0.0)

        q_view = qe1.rearrange("(p n) f -> p n f", n=NT)
        a_view = A.rearrange("(p n) k -> p n k", n=NT)
        o_view = out.rearrange("(p n) f -> p n f", n=NT)
        q_sb = [keep.tile([P, 2, F], BF16, name="q_sb%d" % c) for c in range(NPAIR)]
        a_sb = [keep.tile([P, 2, NK], BF16, name="a_sb%d" % c) for c in range(NPAIR)]
        k_sb = keep.tile([P, 8, F], BF16, name="k_sb")
        v_sb = keep.tile([P, 8, F], BF16, name="v_sb")
        k_view = ke1.rearrange("(j p) f -> p j f", p=P)
        v_view = ve1.rearrange("(j p e) f -> p j e f", p=P, e=2)

        def load_q(c):
            nc.sync.dma_start(out=q_sb[c][:], in_=q_view[:, 2 * c:2 * c + 2, :])

        def load_a(c):
            nc.sync.dma_start(out=a_sb[c][:], in_=a_view[:, 2 * c:2 * c + 2, :])

        def load_a_tile(i):
            nc.sync.dma_start(out=a_sb[i // 2][:, i % 2, :], in_=a_view[:, i, :])

        def load_k(b):
            nc.sync.dma_start(out=k_sb[:, 2 * b:2 * b + 2, :], in_=k_view[:, 2 * b:2 * b + 2, :])

        load_k(0)
        load_k(1)
        load_q(0)
        load_k(2)
        load_k(3)
        load_a_tile(0)
        load_q(1)
        load_a_tile(1)
        load_a_tile(2)
        load_q(2)
        load_a_tile(3)
        nc.sync.dma_start(out=v_sb[:].rearrange("p (j e) f -> p j e f", e=2), in_=v_view)
        load_q(3)
        for c in range(2, NPAIR):
            load_a(c)
            if c + 2 < NPAIR:
                load_q(c + 2)

        k_codes = keep.tile([P, NK], U32, name="k_codes", align_bytes=64)
        k_scales = keep.tile([P, NK], U8, name="k_scales", align_bytes=64)
        v_codes = keep.tile([P, 2 * F], U32, name="v_codes", align_bytes=64)
        v_scales = keep.tile([P, 2 * F], U8, name="v_scales", align_bytes=64)
        q_codes = [keep.tile([P, 2 * P], U32, name="q_codes%d" % j, align_bytes=64) for j in range(NPAIR)]
        q_scales = [keep.tile([P, 2 * P], U8, name="q_scales%d" % j, align_bytes=64) for j in range(NPAIR)]
        kg = keep.tile([P, NK * 4], BF16, name="kg", align_bytes=64)
        vg = keep.tile([P, 2 * F * 4], BF16, name="vg", align_bytes=64)

        def copy_on(eng, dst, src):
            if eng == "v":
                nc.vector.tensor_copy(out=dst, in_=src)
            else:
                nc.scalar.copy(out=dst, in_=src)

        qg = {}
        qt = {}

        def q_transpose(j, borrow=False):
            if borrow:
                qt[j] = ps_o.tile([P, 2, 2, P], F32, name="qt_o", tag="o")
            else:
                qt[j] = ps_qt.tile([P, 2, 2, P], F32, name="qt")
            for a in range(2):
                words = q_sb[j][:, a, :].bitcast(F32)
                for u in range(2):
                    nc.tensor.transpose(qt[j][:, a, u, :], words[:, P * u:P * u + P], ident_f[:])

        def q_evacuate(j, eng):
            qg[j] = work.tile([P, 2 * P * 4], BF16, name="qg", align_bytes=64)
            copy_on(eng, qg[j][:].bitcast(F32).rearrange("p (a q u) -> p a q u", a=2, u=2),
                    qt[j][:].rearrange("p a u q -> p a q u"))

        def q_quantise(j):
            nc.vector.quantize_mx(out=q_codes[j][:].bitcast(FP8X4), scales=q_scales[j][:], in_=qg[j][:])

        kg_words = kg[:].bitcast(F32).rearrange("p (b a k u) -> p b a k u", b=4, a=2, u=2)
        kt = {}

        def k_transpose(b):
            kt[b] = ps_s.tile([P, 2, 2, P], F32, name="kt", tag="s")
            for a in range(2):
                words = k_sb[:, 2 * b + a, :].bitcast(F32)
                for u in range(2):
                    nc.tensor.transpose(kt[b][:, a, u, :], words[:, P * u:P * u + P], ident_f[:])

        def k_evacuate(b, eng):
            copy_on(eng, kg_words[:, b], kt[b][:].rearrange("p a u k -> p a k u"))

        def k_quantise(b):
            nc.vector.quantize_mx(
                out=k_codes[:, 256 * b:256 * b + 256].bitcast(FP8X4),
                scales=k_scales[:, 256 * b:256 * b + 256],
                in_=kg[:, 1024 * b:1024 * b + 1024],
            )

        def v_regroup(g, h, eng):
            c0 = 2048 * g + 1024 * h
            dst = vg[:, c0:c0 + 1024].rearrange("p (c i t) -> p c t i", i=4, t=4)
            src = v_sb[:, 4 * g:4 * g + 4, 256 * h:256 * h + 256].rearrange("p t (c i) -> p c t i", i=4)
            if eng == "g":
                dst = vg[:, c0:c0 + 1024].rearrange("p (f t) -> p f t", t=4)
                src = v_sb[:, 4 * g:4 * g + 4, 256 * h:256 * h + 256].rearrange("p t f -> p f t")
                nc.gpsimd.tensor_scalar(out=dst, in0=src, scalar1=1.0, scalar2=0.0, op0=ALU.mult, op1=ALU.add)
            else:
                copy_on(eng, dst, src)

        def v_quantise(g):
            nc.vector.quantize_mx(
                out=v_codes[:, 512 * g:512 * g + 512].bitcast(FP8X4),
                scales=v_scales[:, 512 * g:512 * g + 512],
                in_=vg[:, 2048 * g:2048 * g + 2048],
            )

        s_ps, m_sb, nmx, rs, e_sb, et_ps, ex = {}, {}, {}, {}, {}, {}, {}
        eg, ec, es, rr, o_ps, o_sb = {}, {}, {}, {}, {}, {}

        def scores(i, g):
            s = ps_s.tile([P, 512], F32, name="s", tag="s")
            nc.tensor.matmul_mx(
                out=s[:],
                lhsT=q_codes[i // 2][:, P * (i % 2):P * (i % 2) + P].bitcast(FP8X4),
                lhsT_scale=q_scales[i // 2][:, P * (i % 2):P * (i % 2) + P],
                rhs=k_codes[:, 512 * g:512 * g + 512].bitcast(FP8X4),
                rhs_scale=k_scales[:, 512 * g:512 * g + 512],
                start=True,
                stop=True,
            )
            s_ps[(i, g)] = s

        def mask(i, g):
            if g == 0:
                m_sb[i] = work.tile([P, W + NK], F32, name="m", bufs=4)
            nc.vector.scalar_tensor_tensor(
                out=m_sb[i][:, W + 512 * g:W + 512 * g + 512],
                in0=s_ps[(i, g)][:],
                scalar=-inv_sqrt_f,
                in1=a_sb[i // 2][:, i % 2, 512 * g:512 * g + 512],
                op0=ALU.mult,
                op1=ALU.mult,
            )

        def mask_off_vector(i, g):
            if g == 0:
                m_sb[i] = work.tile([P, W + NK], F32, name="m", bufs=4)
            raw = small.tile([P, 512], F32, name="raw", bufs=2)
            nc.scalar.activation(out=raw[:], in_=s_ps[(i, g)][:], func=ACT.Copy, scale=-inv_sqrt_f)
            nc.gpsimd.tensor_tensor(out=m_sb[i][:, W + 512 * g:W + 512 * g + 512], in0=raw[:],
                                    in1=a_sb[i // 2][:, i % 2, 512 * g:512 * g + 512], op=ALU.mult)

        def paired(i):
            return 3 <= i < NT - 1

        def pair_min(i):
            a = m_sb[i][:, NK - W:NK]
            b = m_sb[i][:, NK:NK + W]
            d = small.tile([P, W], F32, name="d", bufs=2)
            nc.gpsimd.tensor_tensor(out=d[:], in0=a, in1=b, op=ALU.subtract)
            nc.gpsimd.tensor_scalar(out=d[:], in0=d[:], scalar1=0.0, scalar2=-3.0e38, op0=ALU.min, op1=ALU.max)
            nc.gpsimd.tensor_tensor(out=m_sb[i][:, 0:W], in0=b, in1=d[:], op=ALU.add)

        def row_max(i):
            nmx[i] = small.tile([P, 1], F32, name="nmx")
            nc.vector.tensor_reduce(out=nmx[i][:], in_=m_sb[i][:, 0:NK - W] if paired(i) else m_sb[i][:, W:W + NK], axis=AX.X, op=ALU.min)

        def exponent(i):
            e_sb[i] = work.tile([P, NK], BF16, name="e", bufs=4)
            if i % 2 == 0:
                rs[i // 2] = small.tile([P, 2], F32, name="rs")
            nc.scalar.activation(out=e_sb[i][:], in_=m_sb[i][:, W:W + NK], func=ACT.Exp, bias=nmx[i][:, 0:1], scale=-1.0,
                                 accum_out=rs[i // 2][:, i % 2:i % 2 + 1])

        def exponent_in_halves(i):
            e_sb[i] = work.tile([P, NK], BF16, name="e", bufs=4)
            halves = small.tile([P, 2], F32, name="rs_halves")
            for g in range(2):
                cols = slice(512 * g, 512 * g + 512)
                nc.scalar.activation(out=e_sb[i][:, cols], in_=m_sb[i][:, W + 512 * g:W + 512 * g + 512], func=ACT.Exp, bias=nmx[i][:, 0:1], scale=-1.0,
                                     accum_out=halves[:, g:g + 1])
            return halves

        def join_halves(i, halves):
            nc.vector.tensor_tensor(out=rs[i // 2][:, i % 2:i % 2 + 1], in0=halves[:, 0:1], in1=halves[:, 1:2], op=ALU.add)

        def e_transpose(i):
            et_ps[i] = ps_et.tile([P, 4, P], F32, name="et")
            words = e_sb[i][:].bitcast(F32)
            for w in range(4):
                nc.tensor.transpose(et_ps[i][:, w, :], words[:, P * w:P * w + P], ident_f[:])

        def e_evacuate(i, eng):
            eg[i] = work.tile([P, NK], BF16, name="eg", align_bytes=64, bufs=4)
            copy_on(eng, eg[i][:].bitcast(F32).rearrange("p (g q u) -> p g q u", g=2, u=2),
                    et_ps[i][:].rearrange("p (g u) q -> p g q u", u=2))

        def e_transpose_half(i, g):
            pool, tag = (ps_et, "et") if g == 0 else (ps_qt, "qt")
            et_ps[i, g] = pool.tile([P, 2, P], F32, name="et_half", tag=tag)
            words = e_sb[i][:].bitcast(F32)
            for u in range(2):
                w = 2 * g + u
                nc.tensor.transpose(et_ps[i, g][:, u, :], words[:, P * w:P * w + P], ident_f[:])

        def e_evacuate_half(i, g, eng):
            if g == 0:
                eg[i] = work.tile([P, NK], BF16, name="eg", align_bytes=64, bufs=4)
            copy_on(eng, eg[i][:, 512 * g:512 * g + 512].bitcast(F32).rearrange("p (q u) -> p q u", u=2),
                    et_ps[i, g][:].rearrange("p u q -> p q u"))

        def e_quantise(i, parts=1):
            ec[i] = work.tile([P, 2 * P], U32, name="ec", align_bytes=64)
            es[i] = work.tile([P, 2 * P], U8, name="es", align_bytes=64)
            width = 2 * P // parts
            for h in range(parts):
                cols = slice(width * h, width * h + width)
                nc.vector.quantize_mx(out=ec[i][:, cols].bitcast(FP8X4), scales=es[i][:, cols],
                                      in_=eg[i][:, 4 * width * h:4 * width * h + 4 * width])

        def invert_sums(j):
            rr[j] = small.tile([P, 2], F32, name="rr")
            nc.vector.reciprocal(out=rr[j][:], in_=rs[j][:])

        def weighted_sum(i, banks, borrow=False):
            width = F // banks
            if borrow:
                o_ps[i] = [ps_s.tile([P, width], F32, name="o_s", tag="s") for h in range(banks)]
            else:
                o_ps[i] = [ps_o.tile([P, F], F32, name="o")]
            for g in range(2):
                for h in range(banks):
                    c0 = 512 * g + width * h
                    nc.tensor.matmul_mx(
                        out=o_ps[i][h][:],
                        lhsT=ec[i][:, P * g:P * g + P].bitcast(FP8X4),
                        lhsT_scale=es[i][:, P * g:P * g + P],
                        rhs=v_codes[:, c0:c0 + width].bitcast(FP8X4),
                        rhs_scale=v_scales[:, c0:c0 + width],
                        start=(g == 0),
                        stop=(g == 1),
                    )

        def normalise(i, engines):
            if i % 2 == 0:
                o_sb[i // 2] = outp.tile([P, 2, F], F32, name="o_sb")
            width = F // len(engines)
            for h in range(len(engines)):
                dst = o_sb[i // 2][:, i % 2, width * h:width * h + width]
                if engines[h] == "v":
                    nc.vector.tensor_scalar(out=dst, in0=o_ps[i][h][:], scalar1=rr[i // 2][:, i % 2:i % 2 + 1], scalar2=None, op0=ALU.mult)
                else:
                    nc.scalar.activation(out=dst, in_=o_ps[i][h][:], func=ACT.Copy, scale=rr[i // 2][:, i % 2:i % 2 + 1])

        def store(first, count):
            nc.sync.dma_start(out=o_view[:, first:first + count, :], in_=o_sb[first // 2][:, first % 2:first % 2 + count, :])

        def store_half(i, h):
            nc.sync.dma_start(out=o_view[:, i, 256 * h:256 * h + 256], in_=o_sb[i // 2][:, i % 2, 256 * h:256 * h + 256])

        def live(x):
            return 0 <= x < NT

        for n in range(6):
            idle_out = ps_o.tile([P, F], F32, name="idle_out", tag="o")
            nc.tensor.matmul(idle_out[:], lhsT=idle_in[:, 0:P], rhs=idle_in[:], start=True, stop=True)
        k_transpose(0)
        k_transpose(1)
        q_transpose(0)
        k_evacuate(0, "s")
        k_evacuate(1, "v")
        q_evacuate(0, "s")
        k_quantise(0)
        k_quantise(1)
        q_quantise(0)
        k_transpose(2)
        k_transpose(3)
        scores(0, 0)
        k_evacuate(2, "s")
        k_evacuate(3, "v")
        k_quantise(2)
        k_quantise(3)
        scores(1, 0)
        q_transpose(1)
        mask(0, 0)
        scores(0, 1)
        q_evacuate(1, "s")
        mask_off_vector(1, 0)

        for i in range(NT):
            odd = i % 2 == 1
            if i > 1:
                mask(i, 0)
            if live(i + 1):
                scores(i + 1, 1)
            if i == 0:
                mask_off_vector(1, 1)
            if i != 1:
                mask(i, 1)
            if i == 0:
                q_quantise(1)
            if odd and 2 < (i + 3) // 2 < NPAIR:
                q_quantise((i + 3) // 2)
            if i == 2:
                q_quantise(2)
                v_regroup(1, 0, "g")
                v_regroup(1, 1, "g")
            if i == 3 or i == 4:
                v_quantise(4 - i)
            if live(i - 4):
                e_quantise(i - 4)
                if not odd:
                    invert_sums((i - 4) // 2)
            if paired(i):
                pair_min(i)
            if live(i + 2):
                scores(i + 2, 0)
            if live(i - 2):
                e_transpose(i - 2)
            if i == 0:
                q_transpose(2, borrow=True)
                q_evacuate(2, "s")
            if odd and (i + 5) // 2 < NPAIR:
                q_transpose((i + 5) // 2)
            if live(i - 4):
                weighted_sum(i - 4, 1)
            if i == 0:
                row_max(0)
                exponent(0)
            elif i > 1:
                row_max(i - 1)
                exponent(i - 1)
            if i == 0:
                v_regroup(0, 0, "s")
            if i == 2:
                v_regroup(0, 1, "s")
            if live(i - 2) and i < NT - 1:
                e_evacuate(i - 2, "s")
            if live(i - 4) and i < NT - 1:
                normalise(i - 4, ["s"])
                if (i - 4) % 2 == 1:
                    store(i - 5, 2)
            if odd and (i + 5) // 2 < NPAIR:
                q_evacuate((i + 5) // 2, "s")

        row_max(NT - 1)
        halves = exponent_in_halves(NT - 1)
        normalise(NT - 5, ["s"])
        store(NT - 6, 2)
        e_quantise(NT - 4)
        e_transpose(NT - 2)
        e_evacuate(NT - 3, "v")
        e_transpose_half(NT - 1, 0)
        weighted_sum(NT - 4, 1)
        e_transpose_half(NT - 1, 1)
        invert_sums(NPAIR - 2)
        e_evacuate(NT - 2, "v")
        e_quantise(NT - 3)
        e_evacuate_half(NT - 1, 0, "s")
        e_evacuate_half(NT - 1, 1, "s")
        weighted_sum(NT - 3, 1)
        e_quantise(NT - 2)
        join_halves(NT - 1, halves)
        weighted_sum(NT - 2, 1, borrow=True)
        e_quantise(NT - 1, 2)
        weighted_sum(NT - 1, 2, borrow=True)
        invert_sums(NPAIR - 1)
        normalise(NT - 4, ["s"])
        store(NT - 4, 1)
        normalise(NT - 3, ["v"])
        store(NT - 3, 1)
        normalise(NT - 2, ["s"])
        store(NT - 2, 1)
        normalise(NT - 1, ["v", "s"])
        store_half(NT - 1, 0)
        store_half(NT - 1, 1)
